import numpy as np
import ml_dtypes


def mxq(x, axis, fmt="e4m3"):
    dtype, down = {"e4m3": (ml_dtypes.float8_e4m3fn, 7), "e5m2": (ml_dtypes.float8_e5m2, 14)}[fmt]
    v = np.moveaxis(np.asarray(x, np.float32).astype(ml_dtypes.bfloat16).astype(np.float64), axis, -1)
    blocks = v.reshape(v.shape[:-1] + (-1, 32))
    amax = np.abs(blocks).max(-1, keepdims=True)
    byte = np.maximum(np.where(amax > 0, np.frexp(amax)[1] - 1 + 127, 0) - down, 1)
    scale = np.exp2(byte - 127.0)
    codes = (blocks / scale).astype(np.float32).astype(dtype).astype(np.float64)
    return np.moveaxis((codes * scale).reshape(v.shape), -1, axis)


WIDE = False


def mx_kscale(k):
    if not WIDE:
        return np.ones(k)
    levels = np.array([10, -10, 5, -5, 0])
    a = np.random.permutation(np.resize(levels, k // 512 * 4)).reshape(k // 512, 4)
    idx = np.arange(k)
    return np.exp2(a[idx // 512, idx % 128 // 32])


BF16 = ml_dtypes.bfloat16


def bf(x):
    return np.asarray(x, np.float32).astype(BF16)


def f64(x):
    return np.asarray(x).astype(np.float64)


E2M1 = np.array([0.0, 0.5, 1.0, 1.5, 2.0, 3.0, 4.0, 6.0, -0.0, -0.5, -1.0, -1.5, -2.0, -3.0, -4.0, -6.0])


def pack_weight(w, fmt):
    k, n = w.shape
    w = f64(bf(w)).reshape(k // 32, 32, n)
    amax = np.abs(w).max(1)
    if fmt == "e4m3":
        byte = np.frexp(amax)[1] - 1 + 127 - 7
    else:
        mant, ex = np.frexp(amax / 6.0)
        byte = np.where(mant > 0.5, ex, ex - 1) + 127
    byte = np.clip(np.where(amax > 0, byte, 1), 1, 254)
    scaled = (w * np.exp2(127.0 - byte)[:, None, :]).reshape(k, n).astype(np.float32)
    by_word = np.ascontiguousarray(scaled.reshape(k // 512, 128, 4, n).transpose(0, 1, 3, 2))
    if fmt == "e4m3":
        words = by_word.astype(ml_dtypes.float8_e4m3fn).view(np.uint8)
    else:
        c = by_word.astype(ml_dtypes.float4_e2m1fn).view(np.uint8) & 0xF
        words = c[..., 0::2] | (c[..., 1::2] << 4)
    return np.ascontiguousarray(words), np.ascontiguousarray(byte.astype(np.uint8).reshape(k // 512, 16, n))


def unpack_weight(words, scales, fmt):
    g, p, n, _ = words.shape
    if fmt == "e4m3":
        vals = np.ascontiguousarray(words).view(ml_dtypes.float8_e4m3fn).astype(np.float64)
    else:
        nib = np.empty((g, p, n, 4), np.uint8)
        nib[..., 0::2] = words & 0xF
        nib[..., 1::2] = words >> 4
        vals = E2M1[nib]
    vals = vals * np.repeat(np.exp2(scales.astype(np.float64) - 127.0), 8, axis=1)[..., None]
    return vals.transpose(0, 1, 3, 2).reshape(g * 512, n)


B, C, PS, G, E = 64, 3, 64, 4, 256
NP = G * G
K2 = 2 * E
FMT = "e4m3"


def setup_inputs():
    s = mx_kscale(K2)[:E]
    t = mx_kscale(K2)[:E]
    ss = np.concatenate([s, s])
    tt = np.concatenate([t, t])
    tok = bf(np.random.standard_normal((B, NP, E)) * s)
    corr_w = np.random.standard_normal((E, K2)) / np.sqrt(K2) * t[:, None] / ss[None, :]
    corr_w_words, corr_w_scales = pack_weight(np.ascontiguousarray(corr_w.T), FMT)
    corr_b = bf(np.random.standard_normal(E) * 0.3 * t)
    cross_w = np.random.standard_normal((E, K2)) / np.sqrt(K2) / tt[None, :]
    cross_w_words, cross_w_scales = pack_weight(np.ascontiguousarray(cross_w.T), FMT)
    cross_b = bf(np.random.standard_normal(E) * 0.3)
    return {"tok": tok,
            "corr_w_words": corr_w_words,
            "corr_w_scales": corr_w_scales,
            "corr_b": corr_b,
            "cross_w_words": cross_w_words,
            "cross_w_scales": cross_w_scales,
            "cross_b": cross_b}


def reference(tok, corr_w_words, corr_w_scales, corr_b, cross_w_words, cross_w_scales, cross_b):
    xc = f64(tok)
    a = np.broadcast_to(xc[:, :, None, :], (B, NP, NP, E))
    b = np.broadcast_to(xc[:, None, :, :], (B, NP, NP, E))
    cart = np.concatenate([a, b], axis=-1)
    h = (mxq(cart, 3, "e4m3") @ unpack_weight(corr_w_words, corr_w_scales, FMT)) + f64(corr_b)
    h = h.reshape(B, NP, NP // 2, K2)
    return (mxq(h, 3, "e4m3") @ unpack_weight(cross_w_words, cross_w_scales, FMT)) + f64(cross_b)

@@ -1,0 +1,223 @@
+import concourse.mybir as mybir
+from concourse.masks import make_identity
+
+F32 = mybir.dt.float32
+BF16 = mybir.dt.bfloat16
+I32 = mybir.dt.int32
+U32 = mybir.dt.uint32
+U8 = mybir.dt.uint8
+FP8X4 = mybir.dt.float8_e4m3fn_x4
+IDENTITY = mybir.ActivationFunctionType.Identity
+ADD = mybir.AluOpType.add
+
+P = 128
+HALF = 64
+PACK = 4
+BATCH = 64
+TOKENS = 16
+PAIRS = 8
+EMBED = 256
+GROUP_BATCHES = 16
+GROUPS = BATCH // GROUP_BATCHES
+BLOCK_BATCHES = 4
+BLOCK_ROWS = BLOCK_BATCHES * TOKENS * PAIRS
+BLOCKS = BATCH // BLOCK_BATCHES
+ROW_SETS = BLOCK_ROWS // P
+
+FLOPS = 2 * BATCH * TOKENS * TOKENS * 512 * EMBED + 2 * BATCH * TOKENS * PAIRS * 512 * EMBED
+
+
+def tile_simplemodel_pb_t_kernel(
+    tc, tok, corr_w_words, corr_w_scales, corr_b, cross_w_words, cross_w_scales, cross_b, out
+):
+    nc = tc.nc
+    with tc.tile_pool(name="consts", bufs=1) as consts, tc.tile_pool(name="stage", bufs=2) as stage, tc.tile_pool(
+        name="work", bufs=3
+    ) as work:
+        tok_sb = consts.tile([P, GROUPS, 2 * EMBED], BF16)
+        tok_rows = tok.rearrange("b (m j) e -> (b m) (j e)", j=2)
+        nc.sync.dma_start(out=tok_sb[:, 0, :], in_=tok_rows[0:P, :])
+
+        w1_words = consts.tile([P, 2, 2 * EMBED], I32, align_bytes=64)
+        w1_scales = consts.tile([P, 2, 2 * EMBED], U8, align_bytes=64)
+        w2_words = consts.tile([P, EMBED], I32, align_bytes=64)
+        w2_scales = consts.tile([P, EMBED], U8, align_bytes=64)
+        nc.vector.memset(w1_words[:], 0)
+        nc.vector.memset(w1_scales[:].bitcast(I32), 0)
+        nc.vector.memset(w2_scales[:].bitcast(I32), 0)
+
+        w1_halves = corr_w_words[0].rearrange("p n t -> p (n t)").bitcast(I32).rearrange("(h p) n -> p h n", h=2)
+        s1_rows = corr_w_scales[0].bitcast(I32).rearrange("(h q r) n -> q r h n", h=2, q=2)
+        for j in range(2):
+            nc.sync.dma_start(
+                out=w1_words[HALF * j : HALF * j + HALF, j, :].rearrange("p (h n) -> p h n", h=2), in_=w1_halves
+            )
+        for j in range(2):
+            for q in range(2):
+                first = HALF * j + 32 * q
+                nc.sync.dma_start(
+                    out=w1_scales[first : first + 4, j, :].bitcast(I32).rearrange("r (h n) -> r h n", h=2),
+                    in_=s1_rows[q],
+                )
+        for g in range(1, GROUPS):
+            nc.sync.dma_start(out=tok_sb[:, g, :], in_=tok_rows[P * g : P * g + P, :])
+        nc.sync.dma_start(out=w2_words[:], in_=cross_w_words[0].rearrange("p n t -> p (n t)").bitcast(I32))
+        s2_rows = cross_w_scales[0].bitcast(I32)
+        for q in range(4):
+            nc.sync.dma_start(out=w2_scales[32 * q : 32 * q + 4, :].bitcast(I32), in_=s2_rows[4 * q : 4 * q + 4, :])
+
+        corr_bias_bf = consts.tile([P, PACK], BF16)
+        for half in range(2):
+            nc.scalar.dma_start(
+                out=corr_bias_bf[HALF * half : HALF * half + HALF, :], in_=corr_b.rearrange("(q t) -> q t", t=PACK)
+            )
+        cross_bias_bf = consts.tile([P, 2], BF16)
+        with nc.allow_non_contiguous_dma(reason="256 bias values, one to a partition"):
+            nc.scalar.dma_start(out=cross_bias_bf[:], in_=cross_b.rearrange("(c m) -> m c", c=2))
+        corr_bias = consts.tile([P, PACK], F32)
+        cross_bias = consts.tile([P, 2], F32)
+        nc.vector.tensor_copy(out=corr_bias[:], in_=corr_bias_bf[:])
+        nc.vector.tensor_copy(out=cross_bias[:], in_=cross_bias_bf[:])
+
+        ident = consts.tile([P, P], F32)
+        make_identity(nc, ident[:])
+
+        x_codes = consts.tile([P, GROUPS, P], U32, align_bytes=64)
+        x_scales = consts.tile([P, GROUPS, P], U8, align_bytes=64)
+        a_t = consts.tile([P, PACK, BATCH * TOKENS], F32)
+        b_t = consts.tile([P, BATCH * PAIRS, PACK], F32)
+
+        with tc.psum_pool(name="psum_first", bufs=1) as psum_first:
+            for g in range(GROUPS):
+                tok_t = psum_first.tile([P, 2, P], F32)
+                tok_words = tok_sb[:, g, :].bitcast(F32)
+                for u in range(2):
+                    nc.tensor.transpose(out=tok_t[:, u, :], in_=tok_words[:, u : EMBED : 2], identity=ident[:])
+                grouped = stage.tile([P, P, PACK], BF16, align_bytes=64)
+                nc.scalar.copy(
+                    out=grouped[:].rearrange("p c t -> p (c t)").bitcast(F32).rearrange("p (c u) -> p c u", u=2),
+                    in_=tok_t[:].rearrange("p u c -> p c u"),
+                )
+                nc.vector.quantize_mx(
+                    out=x_codes[:, g, :].bitcast(FP8X4),
+                    scales=x_scales[:, g, :],
+                    in_=grouped[:].rearrange("p c t -> p (c t)"),
+                )
+                a_rows = stage.tile([P, 2, PACK, 2, HALF], F32)
+                b_rows = stage.tile([P, PACK, 2, HALF], F32)
+                for j in range(2):
+                    ab = psum_first.tile([P, 2 * EMBED], F32, name="ab%d" % j)
+                    nc.tensor.matmul_mx(
+                        out=ab[:],
+                        lhsT=x_codes[:, g, :].bitcast(FP8X4),
+                        lhsT_scale=x_scales[:, g, :],
+                        rhs=w1_words[:, j, :].bitcast(FP8X4),
+                        rhs_scale=w1_scales[:, j, :],
+                        start=True,
+                        stop=True,
+                    )
+                    nc.scalar.copy(
+                        out=a_rows[:, j, :, :, :],
+                        in_=ab[:, 0:EMBED]
+                        .rearrange("p (q t) -> p t q", t=PACK)
+                        .unsqueeze(2)
+                        .to_broadcast([P, PACK, 2, HALF]),
+                    )
+                    nc.scalar.copy(
+                        out=b_rows[:, :, j, :], in_=ab[:, EMBED : 2 * EMBED].rearrange("p (q t) -> p t q", t=PACK)
+                    )
+                b_cols = psum_first.tile([P, PACK, P], F32)
+                for t in range(PACK):
+                    nc.tensor.transpose(
+                        out=b_cols[:, t, :], in_=b_rows[:, t, :, :].rearrange("p j q -> p (j q)"), identity=ident[:]
+                    )
+                nc.scalar.copy(out=b_t[:, P * g : P * g + P, :], in_=b_cols[:].rearrange("p t c -> p c t"))
+                for th in range(2):
+                    a_cols = psum_first.tile([P, 2, 2, P], F32, name="a_cols%d" % th)
+                    for tl in range(2):
+                        t = 2 * th + tl
+                        for j in range(2):
+                            nc.tensor.transpose(
+                                out=a_cols[:, tl, j, :],
+                                in_=a_rows[:, j, t, :, :].rearrange("p d q -> p (d q)"),
+                                identity=ident[:],
+                            )
+                        nc.scalar.activation(
+                            out=a_t[:, t, 2 * P * g : 2 * P * g + 2 * P].rearrange("p (c j) -> p c j", j=2),
+                            in_=a_cols[:, tl, :, :].rearrange("p j c -> p c j"),
+                            func=IDENTITY,
+                            bias=corr_bias[:, t : t + 1],
+                            scale=1.0,
+                        )
+
+        h_codes = consts.tile([P, BLOCKS, BLOCK_ROWS], U32, align_bytes=64)
+        h_scales = consts.tile([P, BLOCKS, BLOCK_ROWS], U8, align_bytes=64)
+        out_rows = out.rearrange("b i m n -> (b i m) n")
+
+        with tc.psum_pool(name="psum_second", bufs=4, reuse_waits="tile") as psum_second:
+
+            def add_block(k):
+                h_bf = work.tile([P, BLOCK_ROWS, PACK], BF16, align_bytes=64)
+                for s in range(BLOCK_BATCHES):
+                    b = BLOCK_BATCHES * k + s
+                    shape = [P, TOKENS, PAIRS, PACK]
+                    nc.vector.tensor_tensor(
+                        out=h_bf[:, P * s : P * s + P, :].rearrange("p (i m) t -> p i m t", m=PAIRS),
+                        in0=a_t[:, :, TOKENS * b : TOKENS * b + TOKENS]
+                        .rearrange("p t i -> p i t")
+                        .unsqueeze(2)
+                        .to_broadcast(shape),
+                        in1=b_t[:, PAIRS * b : PAIRS * b + PAIRS, :].unsqueeze(1).to_broadcast(shape),
+                        op=ADD,
+                    )
+                return h_bf
+
+            def finish_block(k, h_bf):
+                nc.vector.quantize_mx(
+                    out=h_codes[:, k, :].bitcast(FP8X4),
+                    scales=h_scales[:, k, :],
+                    in_=h_bf[:].rearrange("p r t -> p (r t)"),
+                )
+                out_t = work.tile([P, 2, ROW_SETS, P], F32)
+                for c in range(2):
+                    acc = psum_second.tile([P, BLOCK_ROWS], F32)
+                    nc.tensor.matmul_mx(
+                        out=acc[:],
+                        lhsT=w2_words[:, P * c : P * c + P].bitcast(FP8X4),
+                        lhsT_scale=w2_scales[:, P * c : P * c + P],
+                        rhs=h_codes[:, k, :].bitcast(FP8X4),
+                        rhs_scale=h_scales[:, k, :],
+                        start=True,
+                        stop=True,
+                    )
+                    nc.scalar.activation(
+                        out=out_t[:, c, :, :],
+                        in_=acc[:].rearrange("p (r s) -> p s r", s=ROW_SETS),
+                        func=IDENTITY,
+                        bias=cross_bias[:, c : c + 1],
+                        scale=1.0,
+                    )
+                result = work.tile([P, ROW_SETS, EMBED], F32)
+                for sh in range(ROW_SETS // 2):
+                    flipped = psum_second.tile([P, 2, EMBED], F32)
+                    for sl in range(2):
+                        for c in range(2):
+                            nc.tensor.transpose(
+                                out=flipped[:, sl, P * c : P * c + P],
+                                in_=out_t[:, c, 2 * sh + sl, :],
+                                identity=ident[:],
+                            )
+                    nc.scalar.copy(out=result[:, 2 * sh : 2 * sh + 2, :], in_=flipped[:])
+                nc.sync.dma_start(
+                    out=out_rows[BLOCK_ROWS * k : BLOCK_ROWS * k + BLOCK_ROWS, :].rearrange(
+                        "(r s) n -> r (s n)", s=ROW_SETS
+                    ),
+                    in_=result[:].rearrange("p s n -> p (s n)"),
+                )
+
+            waiting = add_block(0)
+            for k in range(1, BLOCKS):
+                following = add_block(k)
+                finish_block(k - 1, waiting)
+                waiting = following
+            finish_block(BLOCKS - 1, waiting)

@@ -22,7 +22,12 @@ GROUPS = BATCH // GROUP_BATCHES
 BLOCK_BATCHES = 4
 BLOCK_ROWS = BLOCK_BATCHES * TOKENS * PAIRS
 BLOCKS = BATCH // BLOCK_BATCHES
-ROW_SETS = BLOCK_ROWS // P
+GROUP_BLOCKS = BLOCKS // GROUPS
+PART_ROWS = 256
+BLOCK_PARTS = BLOCK_ROWS // PART_ROWS
+PARTS = BLOCKS * BLOCK_PARTS
+ROW_SETS = PART_ROWS // P
+LAST_PARTS = 8
 
 FLOPS = 2 * BATCH * TOKENS * TOKENS * 512 * EMBED + 2 * BATCH * TOKENS * PAIRS * 512 * EMBED
 
@@ -33,7 +38,9 @@ def tile_simplemodel_pb_t_kernel(
     nc = tc.nc
     with tc.tile_pool(name="consts", bufs=1) as consts, tc.tile_pool(name="stage", bufs=2) as stage, tc.tile_pool(
         name="work", bufs=3
-    ) as work:
+    ) as work, tc.psum_pool(name="psum_b", bufs=1) as psum_b, tc.psum_pool(
+        name="psum", bufs=2
+    ) as psum, tc.manual_schedule():
         tok_sb = consts.tile([P, GROUPS, 2 * EMBED], BF16)
         tok_rows = tok.rearrange("b (m j) e -> (b m) (j e)", j=2)
         nc.sync.dma_start(out=tok_sb[:, 0, :], in_=tok_rows[0:P, :])
@@ -47,11 +54,11 @@ def tile_simplemodel_pb_t_kernel(
         nc.vector.memset(w2_scales[:].bitcast(I32), 0)
 
         w1_halves = corr_w_words[0].rearrange("p n t -> p (n t)").bitcast(I32).rearrange("(h p) n -> p h n", h=2)
-        s1_rows = corr_w_scales[0].bitcast(I32).rearrange("(h q r) n -> q r h n", h=2, q=2)
         for j in range(2):
             nc.sync.dma_start(
                 out=w1_words[HALF * j : HALF * j + HALF, j, :].rearrange("p (h n) -> p h n", h=2), in_=w1_halves
             )
+        s1_rows = corr_w_scales[0].bitcast(I32).rearrange("(h q r) n -> q r h n", h=2, q=2)
         for j in range(2):
             for q in range(2):
                 first = HALF * j + 32 * q
@@ -85,139 +92,177 @@ def tile_simplemodel_pb_t_kernel(
         x_codes = consts.tile([P, GROUPS, P], U32, align_bytes=64)
         x_scales = consts.tile([P, GROUPS, P], U8, align_bytes=64)
         a_t = consts.tile([P, PACK, BATCH * TOKENS], F32)
-        b_t = consts.tile([P, BATCH * PAIRS, PACK], F32)
-
-        with tc.psum_pool(name="psum_first", bufs=1) as psum_first:
-            for g in range(GROUPS):
-                tok_t = psum_first.tile([P, 2, P], F32)
-                tok_words = tok_sb[:, g, :].bitcast(F32)
-                for u in range(2):
-                    nc.tensor.transpose(out=tok_t[:, u, :], in_=tok_words[:, u : EMBED : 2], identity=ident[:])
-                grouped = stage.tile([P, P, PACK], BF16, align_bytes=64)
-                nc.scalar.copy(
-                    out=grouped[:].rearrange("p c t -> p (c t)").bitcast(F32).rearrange("p (c u) -> p c u", u=2),
-                    in_=tok_t[:].rearrange("p u c -> p c u"),
-                )
-                nc.vector.quantize_mx(
-                    out=x_codes[:, g, :].bitcast(FP8X4),
-                    scales=x_scales[:, g, :],
-                    in_=grouped[:].rearrange("p c t -> p (c t)"),
-                )
-                a_rows = stage.tile([P, 2, PACK, 2, HALF], F32)
-                b_rows = stage.tile([P, PACK, 2, HALF], F32)
-                for j in range(2):
-                    ab = psum_first.tile([P, 2 * EMBED], F32, name="ab%d" % j)
-                    nc.tensor.matmul_mx(
-                        out=ab[:],
-                        lhsT=x_codes[:, g, :].bitcast(FP8X4),
-                        lhsT_scale=x_scales[:, g, :],
-                        rhs=w1_words[:, j, :].bitcast(FP8X4),
-                        rhs_scale=w1_scales[:, j, :],
-                        start=True,
-                        stop=True,
-                    )
-                    nc.scalar.copy(
-                        out=a_rows[:, j, :, :, :],
-                        in_=ab[:, 0:EMBED]
-                        .rearrange("p (q t) -> p t q", t=PACK)
-                        .unsqueeze(2)
-                        .to_broadcast([P, PACK, 2, HALF]),
-                    )
-                    nc.scalar.copy(
-                        out=b_rows[:, :, j, :], in_=ab[:, EMBED : 2 * EMBED].rearrange("p (q t) -> p t q", t=PACK)
-                    )
-                b_cols = psum_first.tile([P, PACK, P], F32)
-                for t in range(PACK):
-                    nc.tensor.transpose(
-                        out=b_cols[:, t, :], in_=b_rows[:, t, :, :].rearrange("p j q -> p (j q)"), identity=ident[:]
-                    )
-                nc.scalar.copy(out=b_t[:, P * g : P * g + P, :], in_=b_cols[:].rearrange("p t c -> p c t"))
-                for th in range(2):
-                    a_cols = psum_first.tile([P, 2, 2, P], F32, name="a_cols%d" % th)
-                    for tl in range(2):
-                        t = 2 * th + tl
-                        for j in range(2):
-                            nc.tensor.transpose(
-                                out=a_cols[:, tl, j, :],
-                                in_=a_rows[:, j, t, :, :].rearrange("p d q -> p (d q)"),
-                                identity=ident[:],
-                            )
-                        nc.scalar.activation(
-                            out=a_t[:, t, 2 * P * g : 2 * P * g + 2 * P].rearrange("p (c j) -> p c j", j=2),
-                            in_=a_cols[:, tl, :, :].rearrange("p j c -> p c j"),
-                            func=IDENTITY,
-                            bias=corr_bias[:, t : t + 1],
-                            scale=1.0,
-                        )
-
+        b_cols = [psum_b.tile([P, PACK, P], F32, name="b_cols%d" % g) for g in range(GROUPS)]
+        b_last = consts.tile([P, BLOCKS, PAIRS, PACK], F32)
         h_codes = consts.tile([P, BLOCKS, BLOCK_ROWS], U32, align_bytes=64)
         h_scales = consts.tile([P, BLOCKS, BLOCK_ROWS], U8, align_bytes=64)
         out_rows = out.rearrange("b i m n -> (b i m) n")
 
-        with tc.psum_pool(name="psum_second", bufs=4, reuse_waits="tile") as psum_second:
+        def quantise_tokens(g):
+            tok_t = psum.tile([P, 2, P], F32, tag="flips")
+            tok_words = tok_sb[:, g, :].bitcast(F32)
+            for u in range(2):
+                nc.tensor.transpose(out=tok_t[:, u, :], in_=tok_words[:, u : EMBED : 2], identity=ident[:])
+            grouped = stage.tile([P, P, PACK], BF16, align_bytes=64)
+            nc.scalar.copy(
+                out=grouped[:].rearrange("p c t -> p (c t)").bitcast(F32).rearrange("p (c u) -> p c u", u=2),
+                in_=tok_t[:].rearrange("p u c -> p c u"),
+            )
+            nc.vector.quantize_mx(
+                out=x_codes[:, g, :].bitcast(FP8X4),
+                scales=x_scales[:, g, :],
+                in_=grouped[:].rearrange("p c t -> p (c t)"),
+            )
 
-            def add_block(k):
-                h_bf = work.tile([P, BLOCK_ROWS, PACK], BF16, align_bytes=64)
-                for s in range(BLOCK_BATCHES):
-                    b = BLOCK_BATCHES * k + s
-                    shape = [P, TOKENS, PAIRS, PACK]
+        def first_matmul(g):
+            a_rows = stage.tile([P, 2, PACK, 2, HALF], F32)
+            b_rows = stage.tile([P, PACK, 2, HALF], F32)
+            for j in range(2):
+                ab = psum.tile([P, 2 * EMBED], F32, tag="products")
+                nc.tensor.matmul_mx(
+                    out=ab[:],
+                    lhsT=x_codes[:, g, :].bitcast(FP8X4),
+                    lhsT_scale=x_scales[:, g, :],
+                    rhs=w1_words[:, j, :].bitcast(FP8X4),
+                    rhs_scale=w1_scales[:, j, :],
+                    start=True,
+                    stop=True,
+                )
+                a_spread = (
+                    ab[:, 0:EMBED].rearrange("p (q t) -> p t q", t=PACK).unsqueeze(2).to_broadcast([P, PACK, 2, HALF])
+                )
+                b_spread = ab[:, EMBED : 2 * EMBED].rearrange("p (q t) -> p t q", t=PACK)
+                if g == 0 and j == 0:
+                    nc.vector.tensor_copy(out=b_rows[:, :, j, :], in_=b_spread)
+                    nc.vector.tensor_copy(out=a_rows[:, j, :, :, :], in_=a_spread)
+                else:
+                    nc.scalar.copy(out=b_rows[:, :, j, :], in_=b_spread)
+                    nc.scalar.copy(out=a_rows[:, j, :, :, :], in_=a_spread)
+            for t in range(PACK):
+                nc.tensor.transpose(
+                    out=b_cols[g][:, t, :], in_=b_rows[:, t, :, :].rearrange("p j q -> p (j q)"), identity=ident[:]
+                )
+            for th in range(2):
+                a_cols = psum.tile([P, 2, 2, P], F32, tag="flips")
+                for tl in range(2):
+                    for j in range(2):
+                        nc.tensor.transpose(
+                            out=a_cols[:, tl, j, :],
+                            in_=a_rows[:, j, 2 * th + tl, :, :].rearrange("p d q -> p (d q)"),
+                            identity=ident[:],
+                        )
+                for tl in range(2):
+                    t = 2 * th + tl
+                    a_plane = a_t[:, t, 2 * P * g : 2 * P * g + 2 * P].rearrange("p (c j) -> p c j", j=2)
+                    a_flipped = a_cols[:, tl, :, :].rearrange("p j c -> p c j")
+                    if g == 0 and th == 0:
+                        nc.vector.tensor_scalar_add(out=a_plane, in0=a_flipped, scalar1=corr_bias[:, t : t + 1])
+                    else:
+                        nc.scalar.activation(
+                            out=a_plane, in_=a_flipped, func=IDENTITY, bias=corr_bias[:, t : t + 1], scale=1.0
+                        )
+
+        def add_block(k):
+            h_bf = work.tile([P, BLOCK_ROWS, PACK], BF16, align_bytes=64)
+            shape = [P, TOKENS, PAIRS, PACK]
+            g = k // GROUP_BLOCKS
+            if k % GROUP_BLOCKS == 0:
+                nc.vector.tensor_copy(
+                    out=b_last[:, k : k + GROUP_BLOCKS, :, :],
+                    in_=b_cols[g][:].rearrange("p t (k s m) -> p s k m t", s=BLOCK_BATCHES, m=PAIRS)[
+                        :, BLOCK_BATCHES - 1, :, :, :
+                    ],
+                )
+            for s in range(BLOCK_BATCHES):
+                b = BLOCK_BATCHES * k + s
+                in_group = b % GROUP_BATCHES
+                h_of_b = h_bf[:, P * s : P * s + P, :].rearrange("p (i m) t -> p i m t", m=PAIRS)
+                a_of_b = (
+                    a_t[:, :, TOKENS * b : TOKENS * b + TOKENS]
+                    .rearrange("p t i -> p i t")
+                    .unsqueeze(2)
+                    .to_broadcast(shape)
+                )
+                if s == BLOCK_BATCHES - 1:
+                    nc.gpsimd.tensor_tensor(
+                        out=h_of_b, in0=a_of_b, in1=b_last[:, k, :, :].unsqueeze(1).to_broadcast(shape), op=ADD
+                    )
+                else:
                     nc.vector.tensor_tensor(
-                        out=h_bf[:, P * s : P * s + P, :].rearrange("p (i m) t -> p i m t", m=PAIRS),
-                        in0=a_t[:, :, TOKENS * b : TOKENS * b + TOKENS]
-                        .rearrange("p t i -> p i t")
-                        .unsqueeze(2)
+                        out=h_of_b,
+                        in0=a_of_b,
+                        in1=b_cols[g][:, :, PAIRS * in_group : PAIRS * in_group + PAIRS]
+                        .rearrange("p t m -> p m t")
+                        .unsqueeze(1)
                         .to_broadcast(shape),
-                        in1=b_t[:, PAIRS * b : PAIRS * b + PAIRS, :].unsqueeze(1).to_broadcast(shape),
                         op=ADD,
                     )
-                return h_bf
+            return h_bf
 
-            def finish_block(k, h_bf):
-                nc.vector.quantize_mx(
-                    out=h_codes[:, k, :].bitcast(FP8X4),
-                    scales=h_scales[:, k, :],
-                    in_=h_bf[:].rearrange("p r t -> p (r t)"),
+        def quantise_block(k, h_bf):
+            nc.vector.quantize_mx(
+                out=h_codes[:, k, :].bitcast(FP8X4),
+                scales=h_scales[:, k, :],
+                in_=h_bf[:].rearrange("p r t -> p (r t)"),
+            )
+
+        def second_matmul(part):
+            k = part // BLOCK_PARTS
+            first = PART_ROWS * (part % BLOCK_PARTS)
+            acc = psum.tile([P, 2, PART_ROWS], F32, tag="products")
+            out_t = work.tile([P, 2, ROW_SETS, P], F32)
+            for c in range(2):
+                nc.tensor.matmul_mx(
+                    out=acc[:, c, :],
+                    lhsT=w2_words[:, P * c : P * c + P].bitcast(FP8X4),
+                    lhsT_scale=w2_scales[:, P * c : P * c + P],
+                    rhs=h_codes[:, k, first : first + PART_ROWS].bitcast(FP8X4),
+                    rhs_scale=h_scales[:, k, first : first + PART_ROWS],
+                    start=True,
+                    stop=True,
                 )
-                out_t = work.tile([P, 2, ROW_SETS, P], F32)
+            for c in range(2):
+                nc.scalar.activation(
+                    out=out_t[:, c, :, :],
+                    in_=acc[:, c, :].rearrange("p (r s) -> p s r", s=ROW_SETS),
+                    func=IDENTITY,
+                    bias=cross_bias[:, c : c + 1],
+                    scale=1.0,
+                )
+            return out_t
+
+        def flip_and_store(part, out_t):
+            flipped = psum.tile([P, ROW_SETS, EMBED], F32, tag="flips")
+            for s in range(ROW_SETS):
                 for c in range(2):
-                    acc = psum_second.tile([P, BLOCK_ROWS], F32)
-                    nc.tensor.matmul_mx(
-                        out=acc[:],
-                        lhsT=w2_words[:, P * c : P * c + P].bitcast(FP8X4),
-                        lhsT_scale=w2_scales[:, P * c : P * c + P],
-                        rhs=h_codes[:, k, :].bitcast(FP8X4),
-                        rhs_scale=h_scales[:, k, :],
-                        start=True,
-                        stop=True,
-                    )
-                    nc.scalar.activation(
-                        out=out_t[:, c, :, :],
-                        in_=acc[:].rearrange("p (r s) -> p s r", s=ROW_SETS),
-                        func=IDENTITY,
-                        bias=cross_bias[:, c : c + 1],
-                        scale=1.0,
-                    )
-                result = work.tile([P, ROW_SETS, EMBED], F32)
-                for sh in range(ROW_SETS // 2):
-                    flipped = psum_second.tile([P, 2, EMBED], F32)
-                    for sl in range(2):
-                        for c in range(2):
-                            nc.tensor.transpose(
-                                out=flipped[:, sl, P * c : P * c + P],
-                                in_=out_t[:, c, 2 * sh + sl, :],
-                                identity=ident[:],
-                            )
-                    nc.scalar.copy(out=result[:, 2 * sh : 2 * sh + 2, :], in_=flipped[:])
-                nc.sync.dma_start(
-                    out=out_rows[BLOCK_ROWS * k : BLOCK_ROWS * k + BLOCK_ROWS, :].rearrange(
-                        "(r s) n -> r (s n)", s=ROW_SETS
-                    ),
-                    in_=result[:].rearrange("p s n -> p (s n)"),
-                )
+                    nc.tensor.transpose(out=flipped[:, s, P * c : P * c + P], in_=out_t[:, c, s, :], identity=ident[:])
+            result = work.tile([P, ROW_SETS, EMBED], F32)
+            if part >= PARTS - LAST_PARTS:
+                nc.vector.tensor_copy(out=result[:], in_=flipped[:])
+            else:
+                nc.scalar.copy(out=result[:], in_=flipped[:])
+            nc.sync.dma_start(
+                out=out_rows[PART_ROWS * part : PART_ROWS * part + PART_ROWS, :].rearrange(
+                    "(r s) n -> r (s n)", s=ROW_SETS
+                ),
+                in_=result[:].rearrange("p s n -> p (s n)"),
+            )
 
-            waiting = add_block(0)
-            for k in range(1, BLOCKS):
-                following = add_block(k)
-                finish_block(k - 1, waiting)
-                waiting = following
-            finish_block(BLOCKS - 1, waiting)
+        for g in range(GROUPS):
+            quantise_tokens(g)
+        for g in range(GROUPS):
+            first_matmul(g)
+
+        waiting = add_block(0)
+        for k in range(1, BLOCKS):
+            following = add_block(k)
+            quantise_block(k - 1, waiting)
+            waiting = following
+        quantise_block(BLOCKS - 1, waiting)
+
+        unflipped = second_matmul(0)
+        for part in range(1, PARTS):
+            following = second_matmul(part)
+            flip_and_store(part - 1, unflipped)
+            unflipped = following
+        flip_and_store(PARTS - 1, unflipped)

@@ -23,11 +23,7 @@ BLOCK_BATCHES = 4
 BLOCK_ROWS = BLOCK_BATCHES * TOKENS * PAIRS
 BLOCKS = BATCH // BLOCK_BATCHES
 GROUP_BLOCKS = BLOCKS // GROUPS
-PART_ROWS = 256
-BLOCK_PARTS = BLOCK_ROWS // PART_ROWS
-PARTS = BLOCKS * BLOCK_PARTS
-ROW_SETS = PART_ROWS // P
-LAST_PARTS = 8
+ROW_SETS = BLOCK_ROWS // P
 
 FLOPS = 2 * BATCH * TOKENS * TOKENS * 512 * EMBED + 2 * BATCH * TOKENS * PAIRS * 512 * EMBED
 
@@ -38,9 +34,7 @@ def tile_simplemodel_pb_t_kernel(
     nc = tc.nc
     with tc.tile_pool(name="consts", bufs=1) as consts, tc.tile_pool(name="stage", bufs=2) as stage, tc.tile_pool(
         name="work", bufs=3
-    ) as work, tc.psum_pool(name="psum_b", bufs=1) as psum_b, tc.psum_pool(
-        name="psum", bufs=2
-    ) as psum, tc.manual_schedule():
+    ) as work, tc.psum_pool(name="psum_b", bufs=1) as psum_b, tc.psum_pool(name="psum", bufs=2) as psum:
         tok_sb = consts.tile([P, GROUPS, 2 * EMBED], BF16)
         tok_rows = tok.rearrange("b (m j) e -> (b m) (j e)", j=2)
         nc.sync.dma_start(out=tok_sb[:, 0, :], in_=tok_rows[0:P, :])
@@ -78,11 +72,10 @@ def tile_simplemodel_pb_t_kernel(
             nc.scalar.dma_start(
                 out=corr_bias_bf[HALF * half : HALF * half + HALF, :], in_=corr_b.rearrange("(q t) -> q t", t=PACK)
             )
-        cross_bias_bf = consts.tile([P, 2], BF16)
-        with nc.allow_non_contiguous_dma(reason="256 bias values, one to a partition"):
-            nc.scalar.dma_start(out=cross_bias_bf[:], in_=cross_b.rearrange("(c m) -> m c", c=2))
+        cross_bias_bf = consts.tile([P, EMBED], BF16)
+        nc.scalar.dma_start(out=cross_bias_bf[:], in_=cross_b.partition_broadcast(P))
         corr_bias = consts.tile([P, PACK], F32)
-        cross_bias = consts.tile([P, 2], F32)
+        cross_bias = consts.tile([P, EMBED], F32)
         nc.vector.tensor_copy(out=corr_bias[:], in_=corr_bias_bf[:])
         nc.vector.tensor_copy(out=cross_bias[:], in_=cross_bias_bf[:])
 
@@ -93,7 +86,6 @@ def tile_simplemodel_pb_t_kernel(
         x_scales = consts.tile([P, GROUPS, P], U8, align_bytes=64)
         a_t = consts.tile([P, PACK, BATCH * TOKENS], F32)
         b_cols = [psum_b.tile([P, PACK, P], F32, name="b_cols%d" % g) for g in range(GROUPS)]
-        b_last = consts.tile([P, BLOCKS, PAIRS, PACK], F32)
         h_codes = consts.tile([P, BLOCKS, BLOCK_ROWS], U32, align_bytes=64)
         h_scales = consts.tile([P, BLOCKS, BLOCK_ROWS], U8, align_bytes=64)
         out_rows = out.rearrange("b i m n -> (b i m) n")
@@ -166,13 +158,6 @@ def tile_simplemodel_pb_t_kernel(
             h_bf = work.tile([P, BLOCK_ROWS, PACK], BF16, align_bytes=64)
             shape = [P, TOKENS, PAIRS, PACK]
             g = k // GROUP_BLOCKS
-            if k % GROUP_BLOCKS == 0:
-                nc.vector.tensor_copy(
-                    out=b_last[:, k : k + GROUP_BLOCKS, :, :],
-                    in_=b_cols[g][:].rearrange("p t (k s m) -> p s k m t", s=BLOCK_BATCHES, m=PAIRS)[
-                        :, BLOCK_BATCHES - 1, :, :, :
-                    ],
-                )
             for s in range(BLOCK_BATCHES):
                 b = BLOCK_BATCHES * k + s
                 in_group = b % GROUP_BATCHES
@@ -183,20 +168,15 @@ def tile_simplemodel_pb_t_kernel(
                     .unsqueeze(2)
                     .to_broadcast(shape)
                 )
-                if s == BLOCK_BATCHES - 1:
-                    nc.gpsimd.tensor_tensor(
-                        out=h_of_b, in0=a_of_b, in1=b_last[:, k, :, :].unsqueeze(1).to_broadcast(shape), op=ADD
-                    )
-                else:
-                    nc.vector.tensor_tensor(
-                        out=h_of_b,
-                        in0=a_of_b,
-                        in1=b_cols[g][:, :, PAIRS * in_group : PAIRS * in_group + PAIRS]
-                        .rearrange("p t m -> p m t")
-                        .unsqueeze(1)
-                        .to_broadcast(shape),
-                        op=ADD,
-                    )
+                nc.vector.tensor_tensor(
+                    out=h_of_b,
+                    in0=a_of_b,
+                    in1=b_cols[g][:, :, PAIRS * in_group : PAIRS * in_group + PAIRS]
+                    .rearrange("p t m -> p m t")
+                    .unsqueeze(1)
+                    .to_broadcast(shape),
+                    op=ADD,
+                )
             return h_bf
 
         def quantise_block(k, h_bf):
@@ -206,46 +186,31 @@ def tile_simplemodel_pb_t_kernel(
                 in_=h_bf[:].rearrange("p r t -> p (r t)"),
             )
 
-        def second_matmul(part):
-            k = part // BLOCK_PARTS
-            first = PART_ROWS * (part % BLOCK_PARTS)
-            acc = psum.tile([P, 2, PART_ROWS], F32, tag="products")
-            out_t = work.tile([P, 2, ROW_SETS, P], F32)
-            for c in range(2):
-                nc.tensor.matmul_mx(
-                    out=acc[:, c, :],
-                    lhsT=w2_words[:, P * c : P * c + P].bitcast(FP8X4),
-                    lhsT_scale=w2_scales[:, P * c : P * c + P],
-                    rhs=h_codes[:, k, first : first + PART_ROWS].bitcast(FP8X4),
-                    rhs_scale=h_scales[:, k, first : first + PART_ROWS],
-                    start=True,
-                    stop=True,
-                )
-            for c in range(2):
-                nc.scalar.activation(
-                    out=out_t[:, c, :, :],
-                    in_=acc[:, c, :].rearrange("p (r s) -> p s r", s=ROW_SETS),
-                    func=IDENTITY,
-                    bias=cross_bias[:, c : c + 1],
-                    scale=1.0,
-                )
-            return out_t
-
-        def flip_and_store(part, out_t):
-            flipped = psum.tile([P, ROW_SETS, EMBED], F32, tag="flips")
-            for s in range(ROW_SETS):
-                for c in range(2):
-                    nc.tensor.transpose(out=flipped[:, s, P * c : P * c + P], in_=out_t[:, c, s, :], identity=ident[:])
+        def second_matmul(k):
             result = work.tile([P, ROW_SETS, EMBED], F32)
-            if part >= PARTS - LAST_PARTS:
-                nc.vector.tensor_copy(out=result[:], in_=flipped[:])
-            else:
-                nc.scalar.copy(out=result[:], in_=flipped[:])
+            for sh in range(ROW_SETS // 2):
+                acc = psum.tile([P, 2, EMBED], F32, tag="products")
+                for sl in range(2):
+                    first = P * (2 * sh + sl)
+                    nc.tensor.matmul_mx(
+                        out=acc[:, sl, :],
+                        lhsT=h_codes[:, k, first : first + P].bitcast(FP8X4),
+                        lhsT_scale=h_scales[:, k, first : first + P],
+                        rhs=w2_words[:].bitcast(FP8X4),
+                        rhs_scale=w2_scales[:],
+                        start=True,
+                        stop=True,
+                    )
+                nc.scalar.copy(out=result[:, 2 * sh : 2 * sh + 2, :], in_=acc[:])
+            nc.gpsimd.tensor_tensor(
+                out=result[:],
+                in0=result[:],
+                in1=cross_bias[:].unsqueeze(1).to_broadcast([P, ROW_SETS, EMBED]),
+                op=ADD,
+            )
             nc.sync.dma_start(
-                out=out_rows[PART_ROWS * part : PART_ROWS * part + PART_ROWS, :].rearrange(
-                    "(r s) n -> r (s n)", s=ROW_SETS
-                ),
-                in_=result[:].rearrange("p s n -> p (s n)"),
+                out=out_rows[BLOCK_ROWS * k : BLOCK_ROWS * k + BLOCK_ROWS, :].rearrange("(s r) n -> r s n", s=ROW_SETS),
+                in_=result[:],
             )
 
         for g in range(GROUPS):
@@ -257,12 +222,7 @@ def tile_simplemodel_pb_t_kernel(
         for k in range(1, BLOCKS):
             following = add_block(k)
             quantise_block(k - 1, waiting)
+            second_matmul(k - 1)
             waiting = following
         quantise_block(BLOCKS - 1, waiting)
-
-        unflipped = second_matmul(0)
-        for part in range(1, PARTS):
-            following = second_matmul(part)
-            flip_and_store(part - 1, unflipped)
-            unflipped = following
-        flip_and_store(PARTS - 1, unflipped)
+        second_matmul(BLOCKS - 1)

@@ -23,7 +23,13 @@ BLOCK_BATCHES = 4
 BLOCK_ROWS = BLOCK_BATCHES * TOKENS * PAIRS
 BLOCKS = BATCH // BLOCK_BATCHES
 GROUP_BLOCKS = BLOCKS // GROUPS
-ROW_SETS = BLOCK_ROWS // P
+PART_ROWS = 256
+BLOCK_PARTS = BLOCK_ROWS // PART_ROWS
+PARTS = BLOCKS * BLOCK_PARTS
+ROW_SETS = PART_ROWS // P
+LAST_PARTS = 8
+FIRST_REPEATS = 2
+SECOND_HALVES = (0, 0, 1)
 
 FLOPS = 2 * BATCH * TOKENS * TOKENS * 512 * EMBED + 2 * BATCH * TOKENS * PAIRS * 512 * EMBED
 
@@ -34,7 +40,9 @@ def tile_simplemodel_pb_t_kernel(
     nc = tc.nc
     with tc.tile_pool(name="consts", bufs=1) as consts, tc.tile_pool(name="stage", bufs=2) as stage, tc.tile_pool(
         name="work", bufs=3
-    ) as work, tc.psum_pool(name="psum_b", bufs=1) as psum_b, tc.psum_pool(name="psum", bufs=2) as psum:
+    ) as work, tc.psum_pool(name="psum_b", bufs=1) as psum_b, tc.psum_pool(
+        name="psum", bufs=2
+    ) as psum, tc.manual_schedule():
         tok_sb = consts.tile([P, GROUPS, 2 * EMBED], BF16)
         tok_rows = tok.rearrange("b (m j) e -> (b m) (j e)", j=2)
         nc.sync.dma_start(out=tok_sb[:, 0, :], in_=tok_rows[0:P, :])
@@ -72,10 +80,11 @@ def tile_simplemodel_pb_t_kernel(
             nc.scalar.dma_start(
                 out=corr_bias_bf[HALF * half : HALF * half + HALF, :], in_=corr_b.rearrange("(q t) -> q t", t=PACK)
             )
-        cross_bias_bf = consts.tile([P, EMBED], BF16)
-        nc.scalar.dma_start(out=cross_bias_bf[:], in_=cross_b.partition_broadcast(P))
+        cross_bias_bf = consts.tile([P, 2], BF16)
+        with nc.allow_non_contiguous_dma(reason="256 bias values, one to a partition"):
+            nc.scalar.dma_start(out=cross_bias_bf[:], in_=cross_b.rearrange("(c m) -> m c", c=2))
         corr_bias = consts.tile([P, PACK], F32)
-        cross_bias = consts.tile([P, EMBED], F32)
+        cross_bias = consts.tile([P, 2], F32)
         nc.vector.tensor_copy(out=corr_bias[:], in_=corr_bias_bf[:])
         nc.vector.tensor_copy(out=cross_bias[:], in_=cross_bias_bf[:])
 
@@ -86,6 +95,7 @@ def tile_simplemodel_pb_t_kernel(
         x_scales = consts.tile([P, GROUPS, P], U8, align_bytes=64)
         a_t = consts.tile([P, PACK, BATCH * TOKENS], F32)
         b_cols = [psum_b.tile([P, PACK, P], F32, name="b_cols%d" % g) for g in range(GROUPS)]
+        b_last = consts.tile([P, BLOCKS, PAIRS, PACK], F32)
         h_codes = consts.tile([P, BLOCKS, BLOCK_ROWS], U32, align_bytes=64)
         h_scales = consts.tile([P, BLOCKS, BLOCK_ROWS], U8, align_bytes=64)
         out_rows = out.rearrange("b i m n -> (b i m) n")
@@ -111,15 +121,16 @@ def tile_simplemodel_pb_t_kernel(
             b_rows = stage.tile([P, PACK, 2, HALF], F32)
             for j in range(2):
                 ab = psum.tile([P, 2 * EMBED], F32, tag="products")
-                nc.tensor.matmul_mx(
-                    out=ab[:],
-                    lhsT=x_codes[:, g, :].bitcast(FP8X4),
-                    lhsT_scale=x_scales[:, g, :],
-                    rhs=w1_words[:, j, :].bitcast(FP8X4),
-                    rhs_scale=w1_scales[:, j, :],
-                    start=True,
-                    stop=True,
-                )
+                for repeat in range(FIRST_REPEATS):
+                    nc.tensor.matmul_mx(
+                        out=ab[:],
+                        lhsT=x_codes[:, g, :].bitcast(FP8X4),
+                        lhsT_scale=x_scales[:, g, :],
+                        rhs=w1_words[:, j, :].bitcast(FP8X4),
+                        rhs_scale=w1_scales[:, j, :],
+                        start=True,
+                        stop=True,
+                    )
                 a_spread = (
                     ab[:, 0:EMBED].rearrange("p (q t) -> p t q", t=PACK).unsqueeze(2).to_broadcast([P, PACK, 2, HALF])
                 )
@@ -158,6 +169,13 @@ def tile_simplemodel_pb_t_kernel(
             h_bf = work.tile([P, BLOCK_ROWS, PACK], BF16, align_bytes=64)
             shape = [P, TOKENS, PAIRS, PACK]
             g = k // GROUP_BLOCKS
+            if k % GROUP_BLOCKS == 0:
+                nc.vector.tensor_copy(
+                    out=b_last[:, k : k + GROUP_BLOCKS, :, :],
+                    in_=b_cols[g][:].rearrange("p t (k s m) -> p s k m t", s=BLOCK_BATCHES, m=PAIRS)[
+                        :, BLOCK_BATCHES - 1, :, :, :
+                    ],
+                )
             for s in range(BLOCK_BATCHES):
                 b = BLOCK_BATCHES * k + s
                 in_group = b % GROUP_BATCHES
@@ -168,15 +186,20 @@ def tile_simplemodel_pb_t_kernel(
                     .unsqueeze(2)
                     .to_broadcast(shape)
                 )
-                nc.vector.tensor_tensor(
-                    out=h_of_b,
-                    in0=a_of_b,
-                    in1=b_cols[g][:, :, PAIRS * in_group : PAIRS * in_group + PAIRS]
-                    .rearrange("p t m -> p m t")
-                    .unsqueeze(1)
-                    .to_broadcast(shape),
-                    op=ADD,
-                )
+                if s == BLOCK_BATCHES - 1:
+                    nc.gpsimd.tensor_tensor(
+                        out=h_of_b, in0=a_of_b, in1=b_last[:, k, :, :].unsqueeze(1).to_broadcast(shape), op=ADD
+                    )
+                else:
+                    nc.vector.tensor_tensor(
+                        out=h_of_b,
+                        in0=a_of_b,
+                        in1=b_cols[g][:, :, PAIRS * in_group : PAIRS * in_group + PAIRS]
+                        .rearrange("p t m -> p m t")
+                        .unsqueeze(1)
+                        .to_broadcast(shape),
+                        op=ADD,
+                    )
             return h_bf
 
         def quantise_block(k, h_bf):
@@ -186,31 +209,46 @@ def tile_simplemodel_pb_t_kernel(
                 in_=h_bf[:].rearrange("p r t -> p (r t)"),
             )
 
-        def second_matmul(k):
+        def second_matmul(part):
+            k = part // BLOCK_PARTS
+            first = PART_ROWS * (part % BLOCK_PARTS)
+            acc = psum.tile([P, 2, PART_ROWS], F32, tag="products")
+            out_t = work.tile([P, 2, ROW_SETS, P], F32)
+            for c in SECOND_HALVES:
+                nc.tensor.matmul_mx(
+                    out=acc[:, c, :],
+                    lhsT=w2_words[:, P * c : P * c + P].bitcast(FP8X4),
+                    lhsT_scale=w2_scales[:, P * c : P * c + P],
+                    rhs=h_codes[:, k, first : first + PART_ROWS].bitcast(FP8X4),
+                    rhs_scale=h_scales[:, k, first : first + PART_ROWS],
+                    start=True,
+                    stop=True,
+                )
+            for c in range(2):
+                nc.scalar.activation(
+                    out=out_t[:, c, :, :],
+                    in_=acc[:, c, :].rearrange("p (r s) -> p s r", s=ROW_SETS),
+                    func=IDENTITY,
+                    bias=cross_bias[:, c : c + 1],
+                    scale=1.0,
+                )
+            return out_t
+
+        def flip_and_store(part, out_t):
+            flipped = psum.tile([P, ROW_SETS, EMBED], F32, tag="flips")
+            for s in range(ROW_SETS):
+                for c in range(2):
+                    nc.tensor.transpose(out=flipped[:, s, P * c : P * c + P], in_=out_t[:, c, s, :], identity=ident[:])
             result = work.tile([P, ROW_SETS, EMBED], F32)
-            for sh in range(ROW_SETS // 2):
-                acc = psum.tile([P, 2, EMBED], F32, tag="products")
-                for sl in range(2):
-                    first = P * (2 * sh + sl)
-                    nc.tensor.matmul_mx(
-                        out=acc[:, sl, :],
-                        lhsT=h_codes[:, k, first : first + P].bitcast(FP8X4),
-                        lhsT_scale=h_scales[:, k, first : first + P],
-                        rhs=w2_words[:].bitcast(FP8X4),
-                        rhs_scale=w2_scales[:],
-                        start=True,
-                        stop=True,
-                    )
-                nc.scalar.copy(out=result[:, 2 * sh : 2 * sh + 2, :], in_=acc[:])
-            nc.gpsimd.tensor_tensor(
-                out=result[:],
-                in0=result[:],
-                in1=cross_bias[:].unsqueeze(1).to_broadcast([P, ROW_SETS, EMBED]),
-                op=ADD,
-            )
+            if part >= PARTS - LAST_PARTS:
+                nc.vector.tensor_copy(out=result[:], in_=flipped[:])
+            else:
+                nc.scalar.copy(out=result[:], in_=flipped[:])
             nc.sync.dma_start(
-                out=out_rows[BLOCK_ROWS * k : BLOCK_ROWS * k + BLOCK_ROWS, :].rearrange("(s r) n -> r s n", s=ROW_SETS),
-                in_=result[:],
+                out=out_rows[PART_ROWS * part : PART_ROWS * part + PART_ROWS, :].rearrange(
+                    "(r s) n -> r (s n)", s=ROW_SETS
+                ),
+                in_=result[:].rearrange("p s n -> p (s n)"),
             )
 
         for g in range(GROUPS):
@@ -222,7 +260,12 @@ def tile_simplemodel_pb_t_kernel(
         for k in range(1, BLOCKS):
             following = add_block(k)
             quantise_block(k - 1, waiting)
-            second_matmul(k - 1)
             waiting = following
         quantise_block(BLOCKS - 1, waiting)
-        second_matmul(BLOCKS - 1)
+
+        unflipped = second_matmul(0)
+        for part in range(1, PARTS):
+            following = second_matmul(part)
+            flip_and_store(part - 1, unflipped)
+            unflipped = following
+        flip_and_store(PARTS - 1, unflipped)

@@ -17,19 +17,12 @@ BATCH = 64
 TOKENS = 16
 PAIRS = 8
 EMBED = 256
-GROUP_BATCHES = 16
-GROUPS = BATCH // GROUP_BATCHES
-BLOCK_BATCHES = 4
-BLOCK_ROWS = BLOCK_BATCHES * TOKENS * PAIRS
-BLOCKS = BATCH // BLOCK_BATCHES
-GROUP_BLOCKS = BLOCKS // GROUPS
-PART_ROWS = 256
-BLOCK_PARTS = BLOCK_ROWS // PART_ROWS
-PARTS = BLOCKS * BLOCK_PARTS
-ROW_SETS = PART_ROWS // P
-LAST_PARTS = 8
-FIRST_REPEATS = 2
-SECOND_HALVES = (0, 0, 1)
+CHUNKS = 4
+SETS = 4
+BLOCK = SETS * P
+BLOCKS = 16
+DIRECT = 2
+HALVES = (0, 0, 1)
 
 FLOPS = 2 * BATCH * TOKENS * TOKENS * 512 * EMBED + 2 * BATCH * TOKENS * PAIRS * 512 * EMBED
 
@@ -40,167 +33,122 @@ def tile_simplemodel_pb_t_kernel(
     nc = tc.nc
     with tc.tile_pool(name="consts", bufs=1) as consts, tc.tile_pool(name="stage", bufs=2) as stage, tc.tile_pool(
         name="work", bufs=3
-    ) as work, tc.psum_pool(name="psum_b", bufs=1) as psum_b, tc.psum_pool(
-        name="psum", bufs=2
-    ) as psum, tc.manual_schedule():
-        tok_sb = consts.tile([P, GROUPS, 2 * EMBED], BF16)
-        tok_rows = tok.rearrange("b (m j) e -> (b m) (j e)", j=2)
-        nc.sync.dma_start(out=tok_sb[:, 0, :], in_=tok_rows[0:P, :])
-
-        w1_words = consts.tile([P, 2, 2 * EMBED], I32, align_bytes=64)
-        w1_scales = consts.tile([P, 2, 2 * EMBED], U8, align_bytes=64)
+    ) as work, tc.psum_pool(name="psum", bufs=3) as psum, tc.psum_pool(
+        name="psum_a", bufs=2
+    ) as psum_a, tc.manual_schedule():
+        tok_sb = consts.tile([P, CHUNKS, 2 * EMBED], BF16)
+        tok_rows = tok.rearrange("b (m j) e -> (b m) (j e)", j=2).rearrange("(p c) e -> p c e", c=CHUNKS)
+        w1_raw = consts.tile([P, 2, EMBED], I32, align_bytes=64)
+        s1_raw = consts.tile([P, 2, EMBED], U8, align_bytes=64)
+        w1_words = consts.tile([P, 3, PACK, P], I32, align_bytes=64)
+        s1 = consts.tile([P, 2, PACK, P], U8, align_bytes=64)
         w2_words = consts.tile([P, EMBED], I32, align_bytes=64)
         w2_scales = consts.tile([P, EMBED], U8, align_bytes=64)
-        nc.vector.memset(w1_words[:], 0)
-        nc.vector.memset(w1_scales[:].bitcast(I32), 0)
+        warm = consts.tile([P, 1], F32)
+        nc.vector.memset(warm[:], 0.0)
+        nc.vector.memset(s1_raw[:].bitcast(I32), 0)
         nc.vector.memset(w2_scales[:].bitcast(I32), 0)
+        nc.vector.memset(w1_words[:], 0)
+        warm2 = consts.tile([P, 1], F32)
 
+        nc.sync.dma_start(out=tok_sb[:, 0:2, :], in_=tok_rows[:, 0:2, :])
         w1_halves = corr_w_words[0].rearrange("p n t -> p (n t)").bitcast(I32).rearrange("(h p) n -> p h n", h=2)
         for j in range(2):
-            nc.sync.dma_start(
-                out=w1_words[HALF * j : HALF * j + HALF, j, :].rearrange("p (h n) -> p h n", h=2), in_=w1_halves
-            )
+            nc.sync.dma_start(out=w1_raw[HALF * j : HALF * j + HALF, :, :], in_=w1_halves)
         s1_rows = corr_w_scales[0].bitcast(I32).rearrange("(h q r) n -> q r h n", h=2, q=2)
         for j in range(2):
             for q in range(2):
                 first = HALF * j + 32 * q
-                nc.sync.dma_start(
-                    out=w1_scales[first : first + 4, j, :].bitcast(I32).rearrange("r (h n) -> r h n", h=2),
-                    in_=s1_rows[q],
-                )
-        for g in range(1, GROUPS):
-            nc.sync.dma_start(out=tok_sb[:, g, :], in_=tok_rows[P * g : P * g + P, :])
+                nc.sync.dma_start(out=s1_raw[first : first + 4, :, :].bitcast(I32), in_=s1_rows[q])
+        nc.sync.dma_start(out=tok_sb[:, 2:4, :], in_=tok_rows[:, 2:4, :])
         nc.sync.dma_start(out=w2_words[:], in_=cross_w_words[0].rearrange("p n t -> p (n t)").bitcast(I32))
         s2_rows = cross_w_scales[0].bitcast(I32)
         for q in range(4):
             nc.sync.dma_start(out=w2_scales[32 * q : 32 * q + 4, :].bitcast(I32), in_=s2_rows[4 * q : 4 * q + 4, :])
 
-        corr_bias_bf = consts.tile([P, PACK], BF16)
+        corr_bias = consts.tile([P, PACK], BF16)
         for half in range(2):
             nc.scalar.dma_start(
-                out=corr_bias_bf[HALF * half : HALF * half + HALF, :], in_=corr_b.rearrange("(q t) -> q t", t=PACK)
+                out=corr_bias[HALF * half : HALF * half + HALF, :], in_=corr_b.rearrange("(q t) -> q t", t=PACK)
             )
-        cross_bias_bf = consts.tile([P, 2], BF16)
+        cross_bias = consts.tile([P, 2], BF16)
         with nc.allow_non_contiguous_dma(reason="256 bias values, one to a partition"):
-            nc.scalar.dma_start(out=cross_bias_bf[:], in_=cross_b.rearrange("(c m) -> m c", c=2))
-        corr_bias = consts.tile([P, PACK], F32)
-        cross_bias = consts.tile([P, 2], F32)
-        nc.vector.tensor_copy(out=corr_bias[:], in_=corr_bias_bf[:])
-        nc.vector.tensor_copy(out=cross_bias[:], in_=cross_bias_bf[:])
+            nc.scalar.dma_start(out=cross_bias[:], in_=cross_b.rearrange("(c m) -> m c", c=2))
+        cross_row = consts.tile([P, EMBED], BF16)
+        nc.sync.dma_start(out=cross_row[:], in_=cross_b.partition_broadcast(P))
+        nc.scalar.activation(out=warm2[:], in_=warm[:], func=IDENTITY, bias=0.0, scale=1.0)
 
         ident = consts.tile([P, P], F32)
         make_identity(nc, ident[:])
 
-        x_codes = consts.tile([P, GROUPS, P], U32, align_bytes=64)
-        x_scales = consts.tile([P, GROUPS, P], U8, align_bytes=64)
-        a_t = consts.tile([P, PACK, BATCH * TOKENS], F32)
-        b_cols = [psum_b.tile([P, PACK, P], F32, name="b_cols%d" % g) for g in range(GROUPS)]
-        b_last = consts.tile([P, BLOCKS, PAIRS, PACK], F32)
-        h_codes = consts.tile([P, BLOCKS, BLOCK_ROWS], U32, align_bytes=64)
-        h_scales = consts.tile([P, BLOCKS, BLOCK_ROWS], U8, align_bytes=64)
-        out_rows = out.rearrange("b i m n -> (b i m) n")
+        x_codes = consts.tile([P, CHUNKS * P], U32, align_bytes=64)
+        x_scales = consts.tile([P, CHUNKS * P], U8, align_bytes=64)
+        b_sb = consts.tile([P, 2, CHUNKS, BATCH, PACK], F32)
+        a_sb = consts.tile([P, 3, P, PACK], F32)
+        h_codes = consts.tile([P, BLOCKS, BLOCK], U32, align_bytes=64)
+        h_scales = consts.tile([P, BLOCKS, BLOCK], U8, align_bytes=64)
+        out_rows = out.rearrange("b (l r) m n -> (b l) r (m n)", l=2)
 
-        def quantise_tokens(g):
-            tok_t = psum.tile([P, 2, P], F32, tag="flips")
-            tok_words = tok_sb[:, g, :].bitcast(F32)
-            for u in range(2):
-                nc.tensor.transpose(out=tok_t[:, u, :], in_=tok_words[:, u : EMBED : 2], identity=ident[:])
-            grouped = stage.tile([P, P, PACK], BF16, align_bytes=64)
+        def turn_tokens(half):
+            tok_t = psum.tile([P, 2, 2, P], F32, tag="flips")
+            for k in range(2):
+                words = tok_sb[:, 2 * half + k, :].bitcast(F32)
+                for u in range(2):
+                    nc.tensor.transpose(out=tok_t[:, k, u, :], in_=words[:, u : EMBED : 2], identity=ident[:])
+            grouped = stage.tile([P, 2 * P, PACK], BF16, align_bytes=64)
             nc.scalar.copy(
-                out=grouped[:].rearrange("p c t -> p (c t)").bitcast(F32).rearrange("p (c u) -> p c u", u=2),
-                in_=tok_t[:].rearrange("p u c -> p c u"),
+                out=grouped[:]
+                .rearrange("p n t -> p (n t)")
+                .bitcast(F32)
+                .rearrange("p (k n u) -> p k n u", k=2, u=2),
+                in_=tok_t[:].rearrange("p k u n -> p k n u"),
             )
+            return grouped
+
+        def quantise_tokens(half, grouped):
             nc.vector.quantize_mx(
-                out=x_codes[:, g, :].bitcast(FP8X4),
-                scales=x_scales[:, g, :],
-                in_=grouped[:].rearrange("p c t -> p (c t)"),
+                out=x_codes[:, 2 * P * half : 2 * P * half + 2 * P].bitcast(FP8X4),
+                scales=x_scales[:, 2 * P * half : 2 * P * half + 2 * P],
+                in_=grouped[:].rearrange("p n t -> p (n t)"),
             )
 
-        def first_matmul(g):
-            a_rows = stage.tile([P, 2, PACK, 2, HALF], F32)
-            b_rows = stage.tile([P, PACK, 2, HALF], F32)
-            for j in range(2):
-                ab = psum.tile([P, 2 * EMBED], F32, tag="products")
-                for repeat in range(FIRST_REPEATS):
-                    nc.tensor.matmul_mx(
-                        out=ab[:],
-                        lhsT=x_codes[:, g, :].bitcast(FP8X4),
-                        lhsT_scale=x_scales[:, g, :],
-                        rhs=w1_words[:, j, :].bitcast(FP8X4),
-                        rhs_scale=w1_scales[:, j, :],
-                        start=True,
-                        stop=True,
-                    )
-                a_spread = (
-                    ab[:, 0:EMBED].rearrange("p (q t) -> p t q", t=PACK).unsqueeze(2).to_broadcast([P, PACK, 2, HALF])
-                )
-                b_spread = ab[:, EMBED : 2 * EMBED].rearrange("p (q t) -> p t q", t=PACK)
-                if g == 0 and j == 0:
-                    nc.vector.tensor_copy(out=b_rows[:, :, j, :], in_=b_spread)
-                    nc.vector.tensor_copy(out=a_rows[:, j, :, :, :], in_=a_spread)
-                else:
-                    nc.scalar.copy(out=b_rows[:, :, j, :], in_=b_spread)
-                    nc.scalar.copy(out=a_rows[:, j, :, :, :], in_=a_spread)
+        def first_pass(bank, variant, c):
+            scales = 1 if variant == 2 else 0
             for t in range(PACK):
-                nc.tensor.transpose(
-                    out=b_cols[g][:, t, :], in_=b_rows[:, t, :, :].rearrange("p j q -> p (j q)"), identity=ident[:]
+                nc.tensor.matmul_mx(
+                    out=bank[:, t, :],
+                    lhsT=w1_words[:, variant, t, :].bitcast(FP8X4),
+                    lhsT_scale=s1[:, scales, t, :],
+                    rhs=x_codes[:, P * c : P * c + P].bitcast(FP8X4),
+                    rhs_scale=x_scales[:, P * c : P * c + P],
+                    start=True,
+                    stop=True,
                 )
-            for th in range(2):
-                a_cols = psum.tile([P, 2, 2, P], F32, tag="flips")
-                for tl in range(2):
-                    for j in range(2):
-                        nc.tensor.transpose(
-                            out=a_cols[:, tl, j, :],
-                            in_=a_rows[:, j, 2 * th + tl, :, :].rearrange("p d q -> p (d q)"),
-                            identity=ident[:],
-                        )
-                for tl in range(2):
-                    t = 2 * th + tl
-                    a_plane = a_t[:, t, 2 * P * g : 2 * P * g + 2 * P].rearrange("p (c j) -> p c j", j=2)
-                    a_flipped = a_cols[:, tl, :, :].rearrange("p j c -> p c j")
-                    if g == 0 and th == 0:
-                        nc.vector.tensor_scalar_add(out=a_plane, in0=a_flipped, scalar1=corr_bias[:, t : t + 1])
-                    else:
-                        nc.scalar.activation(
-                            out=a_plane, in_=a_flipped, func=IDENTITY, bias=corr_bias[:, t : t + 1], scale=1.0
-                        )
 
-        def add_block(k):
-            h_bf = work.tile([P, BLOCK_ROWS, PACK], BF16, align_bytes=64)
-            shape = [P, TOKENS, PAIRS, PACK]
-            g = k // GROUP_BLOCKS
-            if k % GROUP_BLOCKS == 0:
-                nc.vector.tensor_copy(
-                    out=b_last[:, k : k + GROUP_BLOCKS, :, :],
-                    in_=b_cols[g][:].rearrange("p t (k s m) -> p s k m t", s=BLOCK_BATCHES, m=PAIRS)[
-                        :, BLOCK_BATCHES - 1, :, :, :
-                    ],
-                )
-            for s in range(BLOCK_BATCHES):
-                b = BLOCK_BATCHES * k + s
-                in_group = b % GROUP_BATCHES
-                h_of_b = h_bf[:, P * s : P * s + P, :].rearrange("p (i m) t -> p i m t", m=PAIRS)
-                a_of_b = (
-                    a_t[:, :, TOKENS * b : TOKENS * b + TOKENS]
-                    .rearrange("p t i -> p i t")
-                    .unsqueeze(2)
-                    .to_broadcast(shape)
-                )
-                if s == BLOCK_BATCHES - 1:
-                    nc.gpsimd.tensor_tensor(
-                        out=h_of_b, in0=a_of_b, in1=b_last[:, k, :, :].unsqueeze(1).to_broadcast(shape), op=ADD
-                    )
-                else:
-                    nc.vector.tensor_tensor(
-                        out=h_of_b,
-                        in0=a_of_b,
-                        in1=b_cols[g][:, :, PAIRS * in_group : PAIRS * in_group + PAIRS]
-                        .rearrange("p t m -> p m t")
-                        .unsqueeze(1)
-                        .to_broadcast(shape),
-                        op=ADD,
-                    )
-            return h_bf
+        def b_part(c):
+            bank = psum.tile([P, PACK, P], F32, tag="acc")
+            first_pass(bank, 2, c)
+            nc.vector.tensor_tensor(
+                out=b_sb[:, :, c, :, :],
+                in0=bank[:].rearrange("p t (b l) -> p l b t", l=2),
+                in1=corr_bias[:].unsqueeze(1).unsqueeze(1).to_broadcast([P, 2, BATCH, PACK]),
+                op=ADD,
+            )
+
+        def a_bank(group):
+            bank = psum_a.tile([P, PACK, P], F32, tag="a")
+            first_pass(bank, group % 2, group // 2)
+            return bank
+
+        shape = [P, BATCH, 2, PACK]
+
+        def add_set(engine, h_bf, s, a_view, l):
+            engine.tensor_tensor(
+                out=h_bf[:, P * s : P * s + P, :].rearrange("p (b l) t -> p b l t", l=2),
+                in0=a_view,
+                in1=b_sb[:, l, s, :, :].unsqueeze(2).to_broadcast(shape),
+                op=ADD,
+            )
 
         def quantise_block(k, h_bf):
             nc.vector.quantize_mx(
@@ -209,63 +157,163 @@ def tile_simplemodel_pb_t_kernel(
                 in_=h_bf[:].rearrange("p r t -> p (r t)"),
             )
 
-        def second_matmul(part):
-            k = part // BLOCK_PARTS
-            first = PART_ROWS * (part % BLOCK_PARTS)
-            acc = psum.tile([P, 2, PART_ROWS], F32, tag="products")
-            out_t = work.tile([P, 2, ROW_SETS, P], F32)
-            for c in SECOND_HALVES:
+        def second_matmul(k):
+            out_t = work.tile([P, 2, BLOCK], F32)
+            accs = [psum.tile([P, BLOCK], F32, tag="acc", name="acc%d" % c) for c in range(2)]
+            for c in HALVES:
                 nc.tensor.matmul_mx(
-                    out=acc[:, c, :],
+                    out=accs[c][:],
                     lhsT=w2_words[:, P * c : P * c + P].bitcast(FP8X4),
                     lhsT_scale=w2_scales[:, P * c : P * c + P],
-                    rhs=h_codes[:, k, first : first + PART_ROWS].bitcast(FP8X4),
-                    rhs_scale=h_scales[:, k, first : first + PART_ROWS],
+                    rhs=h_codes[:, k, :].bitcast(FP8X4),
+                    rhs_scale=h_scales[:, k, :],
                     start=True,
                     stop=True,
                 )
             for c in range(2):
                 nc.scalar.activation(
-                    out=out_t[:, c, :, :],
-                    in_=acc[:, c, :].rearrange("p (r s) -> p s r", s=ROW_SETS),
-                    func=IDENTITY,
-                    bias=cross_bias[:, c : c + 1],
-                    scale=1.0,
+                    out=out_t[:, c, :], in_=accs[c][:], func=IDENTITY, bias=cross_bias[:, c : c + 1], scale=1.0
                 )
             return out_t
 
-        def flip_and_store(part, out_t):
-            flipped = psum.tile([P, ROW_SETS, EMBED], F32, tag="flips")
-            for s in range(ROW_SETS):
-                for c in range(2):
-                    nc.tensor.transpose(out=flipped[:, s, P * c : P * c + P], in_=out_t[:, c, s, :], identity=ident[:])
-            result = work.tile([P, ROW_SETS, EMBED], F32)
-            if part >= PARTS - LAST_PARTS:
-                nc.vector.tensor_copy(out=result[:], in_=flipped[:])
-            else:
-                nc.scalar.copy(out=result[:], in_=flipped[:])
-            nc.sync.dma_start(
-                out=out_rows[PART_ROWS * part : PART_ROWS * part + PART_ROWS, :].rearrange(
-                    "(r s) n -> r (s n)", s=ROW_SETS
-                ),
-                in_=result[:].rearrange("p s n -> p (s n)"),
+        def out_view(k, s0, sets):
+            group, l = block_of[k]
+            r = 2 * (group // 2) + group % 2
+            first = EMBED * (SETS * l + s0)
+            return out_rows[:, r, first : first + EMBED * sets]
+
+        def flip_and_store(k, out_t):
+            result = work.tile([P, SETS, EMBED], F32)
+            for pair in range(2):
+                flipped = psum.tile([P, 2, EMBED], F32, tag="flips")
+                for s in range(2):
+                    for c in range(2):
+                        first = P * (2 * pair + s)
+                        nc.tensor.transpose(
+                            out=flipped[:, s, P * c : P * c + P], in_=out_t[:, c, first : first + P], identity=ident[:]
+                        )
+                nc.scalar.copy(out=result[:, 2 * pair : 2 * pair + 2, :], in_=flipped[:])
+            nc.sync.dma_start(out=out_view(k, 0, SETS), in_=result[:].rearrange("p s n -> p (s n)"))
+
+        def direct_block(k):
+            result = work.tile([P, SETS, EMBED], F32)
+            for pair in range(2):
+                acc = psum.tile([P, 2, EMBED], F32, tag="acc")
+                for s in range(2):
+                    first = P * (2 * pair + s)
+                    nc.tensor.matmul_mx(
+                        out=acc[:, s, :],
+                        lhsT=h_codes[:, k, first : first + P].bitcast(FP8X4),
+                        lhsT_scale=h_scales[:, k, first : first + P],
+                        rhs=w2_words[:].bitcast(FP8X4),
+                        rhs_scale=w2_scales[:],
+                        start=True,
+                        stop=True,
+                    )
+                nc.vector.tensor_tensor(
+                    out=result[:, 2 * pair : 2 * pair + 2, :],
+                    in0=acc[:],
+                    in1=cross_row[:].unsqueeze(1).to_broadcast([P, 2, EMBED]),
+                    op=ADD,
+                )
+                nc.sync.dma_start(
+                    out=out_view(k, 2 * pair, 2), in_=result[:, 2 * pair : 2 * pair + 2, :].rearrange("p s n -> p (s n)")
+                )
+
+        gp_halves = [(g, l) for g in range(3) for l in range(2)]
+        ve_halves = [(g, l) for g in range(3, 8) for l in range(2)] + [gp_halves[5]]
+        block_of = []
+        for k in range(BLOCKS):
+            block_of.append(gp_halves[k // 3] if k % 3 == 2 else ve_halves[k - (k + 1) // 3])
+
+        for j in range(2):
+            rows = slice(HALF * j, HALF * j + HALF)
+            nc.vector.tensor_copy(
+                out=w1_words[rows, 2, :, HALF * j : HALF * j + HALF],
+                in_=w1_raw[rows, 1, :].rearrange("p (q t) -> p t q", t=PACK),
             )
+        nc.vector.tensor_copy(
+            out=s1[:, :, :, 0:HALF].rearrange("p h t q -> p h q t"),
+            in_=s1_raw[:].rearrange("p h (q t) -> p h q t", t=PACK),
+        )
+        s1_ints = s1[:].rearrange("p h t n -> p (h t n)").bitcast(I32).rearrange("p (k d n) -> p k d n", d=2, n=16)
+        nc.vector.tensor_copy(out=s1_ints[:, :, 1, :], in_=s1_ints[:, :, 0, :])
 
-        for g in range(GROUPS):
-            quantise_tokens(g)
-        for g in range(GROUPS):
-            first_matmul(g)
+        first_half = turn_tokens(0)
+        second_half = turn_tokens(1)
+        quantise_tokens(0, first_half)
+        for j in range(2):
+            rows = slice(HALF * j, HALF * j + HALF)
+            nc.vector.tensor_copy(
+                out=w1_words[rows, j, :, :].rearrange("p t (d q) -> p t d q", d=2),
+                in_=w1_raw[rows, 0, :]
+                .rearrange("p (q t) -> p t q", t=PACK)
+                .unsqueeze(2)
+                .to_broadcast([HALF, PACK, 2, HALF]),
+            )
+        quantise_tokens(1, second_half)
+        b_part(0)
+        b_part(1)
+        b_part(2)
+        b_part(3)
 
-        waiting = add_block(0)
-        for k in range(1, BLOCKS):
-            following = add_block(k)
-            quantise_block(k - 1, waiting)
-            waiting = following
-        quantise_block(BLOCKS - 1, waiting)
+        def gp_group(g):
+            bank = a_bank(g)
+            nc.scalar.copy(out=a_sb[:, g, :, :], in_=bank[:].rearrange("p t n -> p n t"))
 
-        unflipped = second_matmul(0)
-        for part in range(1, PARTS):
-            following = second_matmul(part)
-            flip_and_store(part - 1, unflipped)
-            unflipped = following
-        flip_and_store(PARTS - 1, unflipped)
+        gp_group(0)
+        banks = {}
+        banks[3] = a_bank(3)
+        waiting = []
+        unflipped = []
+
+        def finish(k):
+            if k >= BLOCKS - DIRECT:
+                if unflipped:
+                    flip_and_store(*unflipped.pop())
+                direct_block(k)
+                return
+            following = second_matmul(k)
+            if unflipped:
+                flip_and_store(*unflipped.pop())
+            unflipped.append((k, following))
+
+        tiles = {}
+        for k in range(BLOCKS):
+            if k % 3 == 0 and k + 2 < BLOCKS:
+                j = k // 3
+                group, l = gp_halves[j]
+                h_gp = work.tile([P, BLOCK, PACK], BF16, align_bytes=64)
+                for s in range(SETS):
+                    add_set(
+                        nc.gpsimd, h_gp, s, a_sb[:, group, :, :].rearrange("p (b l) t -> p b l t", l=2), l
+                    )
+                tiles[k + 2] = h_gp
+                if j == 0:
+                    gp_group(1)
+                if j == 1:
+                    gp_group(2)
+            if k % 3 == 2:
+                waiting.append(k)
+                continue
+            group, l = block_of[k]
+            h_ve = work.tile([P, BLOCK, PACK], BF16, align_bytes=64)
+            tiles[k] = h_ve
+            for s in range(SETS):
+                add_set(
+                    nc.vector, h_ve, s, banks[group][:].rearrange("p t (b l) -> p b l t", l=2), l
+                )
+            if l == 0 and group + 1 < 8:
+                banks[group + 1] = a_bank(group + 1)
+            if group == 7 and l == 0:
+                banks[2] = a_bank(2)
+            for w in waiting:
+                quantise_block(w, tiles[w])
+            for w in waiting:
+                finish(w)
+            waiting = [k]
+        for w in waiting:
+            quantise_block(w, tiles[w])
+            finish(w)
+        if unflipped:
+            flip_and_store(*unflipped.pop())

@@ -21,7 +21,7 @@ CHUNKS = 4
 SETS = 4
 BLOCK = SETS * P
 BLOCKS = 16
-DIRECT = 2
+DIRECT = 3
 HALVES = (0, 0, 1)
 
 FLOPS = 2 * BATCH * TOKENS * TOKENS * 512 * EMBED + 2 * BATCH * TOKENS * PAIRS * 512 * EMBED
@@ -31,10 +31,14 @@ def tile_simplemodel_pb_t_kernel(
     tc, tok, corr_w_words, corr_w_scales, corr_b, cross_w_words, cross_w_scales, cross_b, out
 ):
     nc = tc.nc
-    with tc.tile_pool(name="consts", bufs=1) as consts, tc.tile_pool(name="stage", bufs=2) as stage, tc.tile_pool(
+    with tc.tile_pool(name="consts", bufs=1) as consts, tc.tile_pool(name="stage", bufs=3) as stage, tc.tile_pool(
         name="work", bufs=3
-    ) as work, tc.psum_pool(name="psum", bufs=3) as psum, tc.psum_pool(
-        name="psum_a", bufs=2
+    ) as work, tc.tile_pool(name="results", bufs=6) as results, tc.psum_pool(
+        name="psum_acc", bufs=3
+    ) as psum_acc, tc.psum_pool(
+        name="psum_flips", bufs=2
+    ) as psum_flips, tc.psum_pool(
+        name="psum_a", bufs=3
     ) as psum_a, tc.manual_schedule():
         tok_sb = consts.tile([P, CHUNKS, 2 * EMBED], BF16)
         tok_rows = tok.rearrange("b (m j) e -> (b m) (j e)", j=2).rearrange("(p c) e -> p c e", c=CHUNKS)
@@ -44,22 +48,22 @@ def tile_simplemodel_pb_t_kernel(
         s1 = consts.tile([P, 2, PACK, P], U8, align_bytes=64)
         w2_words = consts.tile([P, EMBED], I32, align_bytes=64)
         w2_scales = consts.tile([P, EMBED], U8, align_bytes=64)
-        warm = consts.tile([P, 1], F32)
-        nc.vector.memset(warm[:], 0.0)
+        warm = consts.tile([P, 2], F32)
         nc.vector.memset(s1_raw[:].bitcast(I32), 0)
-        nc.vector.memset(w2_scales[:].bitcast(I32), 0)
+        nc.vector.memset(warm[:], 0.0)
         nc.vector.memset(w1_words[:], 0)
-        warm2 = consts.tile([P, 1], F32)
+        nc.vector.memset(w2_scales[:].bitcast(I32), 0)
 
-        nc.sync.dma_start(out=tok_sb[:, 0:2, :], in_=tok_rows[:, 0:2, :])
         w1_halves = corr_w_words[0].rearrange("p n t -> p (n t)").bitcast(I32).rearrange("(h p) n -> p h n", h=2)
         for j in range(2):
             nc.sync.dma_start(out=w1_raw[HALF * j : HALF * j + HALF, :, :], in_=w1_halves)
+        nc.sync.dma_start(out=tok_sb[:, 0, :], in_=tok_rows[:, 0, :])
         s1_rows = corr_w_scales[0].bitcast(I32).rearrange("(h q r) n -> q r h n", h=2, q=2)
         for j in range(2):
             for q in range(2):
                 first = HALF * j + 32 * q
                 nc.sync.dma_start(out=s1_raw[first : first + 4, :, :].bitcast(I32), in_=s1_rows[q])
+        nc.sync.dma_start(out=tok_sb[:, 1, :], in_=tok_rows[:, 1, :])
         nc.sync.dma_start(out=tok_sb[:, 2:4, :], in_=tok_rows[:, 2:4, :])
         nc.sync.dma_start(out=w2_words[:], in_=cross_w_words[0].rearrange("p n t -> p (n t)").bitcast(I32))
         s2_rows = cross_w_scales[0].bitcast(I32)
@@ -76,40 +80,42 @@ def tile_simplemodel_pb_t_kernel(
             nc.scalar.dma_start(out=cross_bias[:], in_=cross_b.rearrange("(c m) -> m c", c=2))
         cross_row = consts.tile([P, EMBED], BF16)
         nc.sync.dma_start(out=cross_row[:], in_=cross_b.partition_broadcast(P))
-        nc.scalar.activation(out=warm2[:], in_=warm[:], func=IDENTITY, bias=0.0, scale=1.0)
+        nc.scalar.activation(out=warm[:, 1:2], in_=warm[:, 0:1], func=IDENTITY, bias=0.0, scale=1.0)
 
         ident = consts.tile([P, P], F32)
         make_identity(nc, ident[:])
 
         x_codes = consts.tile([P, CHUNKS * P], U32, align_bytes=64)
         x_scales = consts.tile([P, CHUNKS * P], U8, align_bytes=64)
-        b_sb = consts.tile([P, 2, CHUNKS, BATCH, PACK], F32)
-        a_sb = consts.tile([P, 3, P, PACK], F32)
+        b_sb = consts.tile([P, CHUNKS, 2, BATCH, PACK], F32)
+        a_sb = consts.tile([P, 8, P, PACK], F32)
         h_codes = consts.tile([P, BLOCKS, BLOCK], U32, align_bytes=64)
         h_scales = consts.tile([P, BLOCKS, BLOCK], U8, align_bytes=64)
         out_rows = out.rearrange("b (l r) m n -> (b l) r (m n)", l=2)
 
-        def turn_tokens(half):
-            tok_t = psum.tile([P, 2, 2, P], F32, tag="flips")
-            for k in range(2):
-                words = tok_sb[:, 2 * half + k, :].bitcast(F32)
+        def turn_tokens(chunks):
+            n = len(chunks)
+            tok_t = psum_flips.tile([P, 2, 2, P], F32, tag="flips")
+            for k in range(n):
+                words = tok_sb[:, chunks[k], :].bitcast(F32)
                 for u in range(2):
                     nc.tensor.transpose(out=tok_t[:, k, u, :], in_=words[:, u : EMBED : 2], identity=ident[:])
             grouped = stage.tile([P, 2 * P, PACK], BF16, align_bytes=64)
             nc.scalar.copy(
-                out=grouped[:]
+                out=grouped[:, 0 : n * P, :]
                 .rearrange("p n t -> p (n t)")
                 .bitcast(F32)
-                .rearrange("p (k n u) -> p k n u", k=2, u=2),
-                in_=tok_t[:].rearrange("p k u n -> p k n u"),
+                .rearrange("p (k n u) -> p k n u", k=n, u=2),
+                in_=tok_t[:, 0:n, :, :].rearrange("p k u n -> p k n u"),
             )
             return grouped
 
-        def quantise_tokens(half, grouped):
+        def quantise_tokens(chunks, grouped):
+            cols = slice(P * chunks[0], P * chunks[0] + P * len(chunks))
             nc.vector.quantize_mx(
-                out=x_codes[:, 2 * P * half : 2 * P * half + 2 * P].bitcast(FP8X4),
-                scales=x_scales[:, 2 * P * half : 2 * P * half + 2 * P],
-                in_=grouped[:].rearrange("p n t -> p (n t)"),
+                out=x_codes[:, cols].bitcast(FP8X4),
+                scales=x_scales[:, cols],
+                in_=grouped[:, 0 : P * len(chunks), :].rearrange("p n t -> p (n t)"),
             )
 
         def first_pass(bank, variant, c):
@@ -125,84 +131,104 @@ def tile_simplemodel_pb_t_kernel(
                     stop=True,
                 )
 
-        def b_part(c):
-            bank = psum.tile([P, PACK, P], F32, tag="acc")
+        def b_pass(c):
+            bank = psum_acc.tile([P, PACK, P], F32, tag="acc")
             first_pass(bank, 2, c)
+            return bank
+
+        def b_add(c, bank):
             nc.vector.tensor_tensor(
-                out=b_sb[:, :, c, :, :],
+                out=b_sb[:, c, :, :, :],
                 in0=bank[:].rearrange("p t (b l) -> p l b t", l=2),
                 in1=corr_bias[:].unsqueeze(1).unsqueeze(1).to_broadcast([P, 2, BATCH, PACK]),
                 op=ADD,
             )
 
-        def a_bank(group):
+        def a_pass(group):
             bank = psum_a.tile([P, PACK, P], F32, tag="a")
             first_pass(bank, group % 2, group // 2)
             return bank
 
-        shape = [P, BATCH, 2, PACK]
+        def a_copy(group):
+            bank = psum_acc.tile([P, PACK, P], F32, tag="acc")
+            first_pass(bank, group % 2, group // 2)
+            nc.scalar.copy(out=a_sb[:, group, :, :], in_=bank[:].rearrange("p t n -> p n t"))
 
-        def add_set(engine, h_bf, s, a_view, l):
+        def add_sets(engine, h, a_view, first_set, sets):
+            shape = [P, sets, BATCH, 2, PACK]
+            b_view = b_sb[:].rearrange("p c l b t -> p (c l) b t")[:, first_set : first_set + sets, :, :]
             engine.tensor_tensor(
-                out=h_bf[:, P * s : P * s + P, :].rearrange("p (b l) t -> p b l t", l=2),
-                in0=a_view,
-                in1=b_sb[:, l, s, :, :].unsqueeze(2).to_broadcast(shape),
+                out=h.rearrange("p (s b l) t -> p s b l t", l=2, b=BATCH),
+                in0=a_view.unsqueeze(1).to_broadcast(shape),
+                in1=b_view.unsqueeze(3).to_broadcast(shape),
                 op=ADD,
             )
 
-        def quantise_block(k, h_bf):
+        def quantise(first, h):
+            flat_codes = h_codes[:].rearrange("p k n -> p (k n)")
+            flat_scales = h_scales[:].rearrange("p k n -> p (k n)")
+            n = h.shape[1]
             nc.vector.quantize_mx(
-                out=h_codes[:, k, :].bitcast(FP8X4),
-                scales=h_scales[:, k, :],
-                in_=h_bf[:].rearrange("p r t -> p (r t)"),
+                out=flat_codes[:, first : first + n].bitcast(FP8X4),
+                scales=flat_scales[:, first : first + n],
+                in_=h.rearrange("p r t -> p (r t)"),
             )
 
-        def second_matmul(k):
+        def out_view(group, c, chunks):
+            r = 2 * (group // 2) + group % 2
+            view = out_rows[:, r, :].rearrange("p (l c n) -> p l c n", l=2, c=CHUNKS)
+            return view[:, :, c : c + chunks, :].rearrange("p l c n -> p l (c n)")
+
+        def second_matmul(k, first, rows):
             out_t = work.tile([P, 2, BLOCK], F32)
-            accs = [psum.tile([P, BLOCK], F32, tag="acc", name="acc%d" % c) for c in range(2)]
+            if rows == BLOCK:
+                accs = [psum_acc.tile([P, BLOCK], F32, tag="acc", name="acc%d" % c)[:] for c in range(2)]
+            else:
+                both = psum_acc.tile([P, 2, rows], F32, tag="acc")
+                accs = [both[:, c, :] for c in range(2)]
             for c in HALVES:
                 nc.tensor.matmul_mx(
-                    out=accs[c][:],
+                    out=accs[c],
                     lhsT=w2_words[:, P * c : P * c + P].bitcast(FP8X4),
                     lhsT_scale=w2_scales[:, P * c : P * c + P],
-                    rhs=h_codes[:, k, :].bitcast(FP8X4),
-                    rhs_scale=h_scales[:, k, :],
+                    rhs=h_codes[:, k, first : first + rows].bitcast(FP8X4),
+                    rhs_scale=h_scales[:, k, first : first + rows],
                     start=True,
                     stop=True,
                 )
             for c in range(2):
                 nc.scalar.activation(
-                    out=out_t[:, c, :], in_=accs[c][:], func=IDENTITY, bias=cross_bias[:, c : c + 1], scale=1.0
+                    out=out_t[:, c, 0:rows], in_=accs[c], func=IDENTITY, bias=cross_bias[:, c : c + 1], scale=1.0
                 )
             return out_t
 
-        def out_view(k, s0, sets):
-            group, l = block_of[k]
-            r = 2 * (group // 2) + group % 2
-            first = EMBED * (SETS * l + s0)
-            return out_rows[:, r, first : first + EMBED * sets]
-
-        def flip_and_store(k, out_t):
-            result = work.tile([P, SETS, EMBED], F32)
-            for pair in range(2):
-                flipped = psum.tile([P, 2, EMBED], F32, tag="flips")
-                for s in range(2):
+        def flip_and_store(k, first, rows, out_t):
+            group, ch = block_of[k]
+            chunks = rows // (2 * P)
+            c0 = 2 * ch + first // (2 * P)
+            result = results.tile([P, 2, 2, EMBED], F32)
+            for chunk in range(chunks):
+                flipped = psum_flips.tile([P, 2, EMBED], F32, tag="flips")
+                for l in range(2):
                     for c in range(2):
-                        first = P * (2 * pair + s)
+                        col = P * (2 * chunk + l)
                         nc.tensor.transpose(
-                            out=flipped[:, s, P * c : P * c + P], in_=out_t[:, c, first : first + P], identity=ident[:]
+                            out=flipped[:, l, P * c : P * c + P], in_=out_t[:, c, col : col + P], identity=ident[:]
                         )
-                nc.scalar.copy(out=result[:, 2 * pair : 2 * pair + 2, :], in_=flipped[:])
-            nc.sync.dma_start(out=out_view(k, 0, SETS), in_=result[:].rearrange("p s n -> p (s n)"))
+                nc.scalar.copy(out=result[:, :, chunk, :], in_=flipped[:])
+            nc.sync.dma_start(
+                out=out_view(group, c0, chunks), in_=result[:, :, 0:chunks, :].rearrange("p l c n -> p l (c n)")
+            )
 
         def direct_block(k):
-            result = work.tile([P, SETS, EMBED], F32)
-            for pair in range(2):
-                acc = psum.tile([P, 2, EMBED], F32, tag="acc")
-                for s in range(2):
-                    first = P * (2 * pair + s)
+            group, ch = block_of[k]
+            result = results.tile([P, 2, 2, EMBED], F32)
+            for chunk in range(2):
+                acc = psum_a.tile([P, 2, EMBED], F32, tag="a")
+                for l in range(2):
+                    first = P * (2 * chunk + l)
                     nc.tensor.matmul_mx(
-                        out=acc[:, s, :],
+                        out=acc[:, l, :],
                         lhsT=h_codes[:, k, first : first + P].bitcast(FP8X4),
                         lhsT_scale=h_scales[:, k, first : first + P],
                         rhs=w2_words[:].bitcast(FP8X4),
@@ -211,109 +237,132 @@ def tile_simplemodel_pb_t_kernel(
                         stop=True,
                     )
                 nc.vector.tensor_tensor(
-                    out=result[:, 2 * pair : 2 * pair + 2, :],
+                    out=result[:, :, chunk, :],
                     in0=acc[:],
                     in1=cross_row[:].unsqueeze(1).to_broadcast([P, 2, EMBED]),
                     op=ADD,
                 )
-                nc.sync.dma_start(
-                    out=out_view(k, 2 * pair, 2), in_=result[:, 2 * pair : 2 * pair + 2, :].rearrange("p s n -> p (s n)")
+                nc.sync.dma_start(out=out_view(group, 2 * ch + chunk, 1), in_=result[:, :, chunk, :])
+
+        VE_GROUPS = [0, 3, 4, 5, 6, 7]
+        ve = [(g, ch) for g in VE_GROUPS for ch in range(2)][0:11]
+        gp = [(2, 0), (2, 1), (1, 0), (1, 1), (7, 1)]
+        block_of = [ve[0]]
+        for j in range(5):
+            block_of += [ve[2 * j + 1], gp[j], ve[2 * j + 2]]
+
+        def sort_columns(variant, h, rows, cols, dup):
+            view = w1_raw[rows, h, :].rearrange("p (q t) -> p t q", t=PACK)
+            if dup:
+                nc.vector.tensor_copy(
+                    out=w1_words[rows, variant, :, :].rearrange("p t (d q) -> p t d q", d=2),
+                    in_=view.unsqueeze(2).to_broadcast([HALF, PACK, 2, HALF]),
                 )
+            else:
+                nc.vector.tensor_copy(out=w1_words[rows, variant, :, cols], in_=view)
 
-        gp_halves = [(g, l) for g in range(3) for l in range(2)]
-        ve_halves = [(g, l) for g in range(3, 8) for l in range(2)] + [gp_halves[5]]
-        block_of = []
-        for k in range(BLOCKS):
-            block_of.append(gp_halves[k // 3] if k % 3 == 2 else ve_halves[k - (k + 1) // 3])
+        low, high = slice(0, HALF), slice(HALF, P)
+        tok0 = turn_tokens([0])
+        tok1 = turn_tokens([1])
+        tok23 = turn_tokens([2, 3])
 
-        for j in range(2):
-            rows = slice(HALF * j, HALF * j + HALF)
-            nc.vector.tensor_copy(
-                out=w1_words[rows, 2, :, HALF * j : HALF * j + HALF],
-                in_=w1_raw[rows, 1, :].rearrange("p (q t) -> p t q", t=PACK),
-            )
+        sort_columns(2, 1, low, low, False)
+        sort_columns(2, 1, high, high, False)
         nc.vector.tensor_copy(
             out=s1[:, :, :, 0:HALF].rearrange("p h t q -> p h q t"),
             in_=s1_raw[:].rearrange("p h (q t) -> p h q t", t=PACK),
         )
         s1_ints = s1[:].rearrange("p h t n -> p (h t n)").bitcast(I32).rearrange("p (k d n) -> p k d n", d=2, n=16)
         nc.vector.tensor_copy(out=s1_ints[:, :, 1, :], in_=s1_ints[:, :, 0, :])
+        sort_columns(0, 0, low, None, True)
 
-        first_half = turn_tokens(0)
-        second_half = turn_tokens(1)
-        quantise_tokens(0, first_half)
-        for j in range(2):
-            rows = slice(HALF * j, HALF * j + HALF)
-            nc.vector.tensor_copy(
-                out=w1_words[rows, j, :, :].rearrange("p t (d q) -> p t d q", d=2),
-                in_=w1_raw[rows, 0, :]
-                .rearrange("p (q t) -> p t q", t=PACK)
-                .unsqueeze(2)
-                .to_broadcast([HALF, PACK, 2, HALF]),
-            )
-        quantise_tokens(1, second_half)
-        b_part(0)
-        b_part(1)
-        b_part(2)
-        b_part(3)
-
-        def gp_group(g):
-            bank = a_bank(g)
-            nc.scalar.copy(out=a_sb[:, g, :, :], in_=bank[:].rearrange("p t n -> p n t"))
-
-        gp_group(0)
         banks = {}
-        banks[3] = a_bank(3)
-        waiting = []
+
+        def a_view(group):
+            return banks[group][:].rearrange("p t (b l) -> p b l t", l=2)
+
         unflipped = []
 
-        def finish(k):
-            if k >= BLOCKS - DIRECT:
-                if unflipped:
-                    flip_and_store(*unflipped.pop())
-                direct_block(k)
-                return
-            following = second_matmul(k)
+        def flush():
             if unflipped:
                 flip_and_store(*unflipped.pop())
-            unflipped.append((k, following))
 
-        tiles = {}
-        for k in range(BLOCKS):
-            if k % 3 == 0 and k + 2 < BLOCKS:
-                j = k // 3
-                group, l = gp_halves[j]
-                h_gp = work.tile([P, BLOCK, PACK], BF16, align_bytes=64)
-                for s in range(SETS):
-                    add_set(
-                        nc.gpsimd, h_gp, s, a_sb[:, group, :, :].rearrange("p (b l) t -> p b l t", l=2), l
-                    )
-                tiles[k + 2] = h_gp
-                if j == 0:
-                    gp_group(1)
-                if j == 1:
-                    gp_group(2)
-            if k % 3 == 2:
-                waiting.append(k)
-                continue
-            group, l = block_of[k]
-            h_ve = work.tile([P, BLOCK, PACK], BF16, align_bytes=64)
-            tiles[k] = h_ve
+        def scalar_out(k, first=0, rows=BLOCK):
+            out_t = second_matmul(k, first, rows)
+            flush()
+            unflipped.append((k, first, rows, out_t))
+
+        def gp_block(j, h):
+            group, ch = gp[j]
+            view = a_sb[:, group, :, :].rearrange("p (b l) t -> p b l t", l=2)
             for s in range(SETS):
-                add_set(
-                    nc.vector, h_ve, s, banks[group][:].rearrange("p t (b l) -> p b l t", l=2), l
-                )
-            if l == 0 and group + 1 < 8:
-                banks[group + 1] = a_bank(group + 1)
-            if group == 7 and l == 0:
-                banks[2] = a_bank(2)
-            for w in waiting:
-                quantise_block(w, tiles[w])
-            for w in waiting:
-                finish(w)
-            waiting = [k]
-        for w in waiting:
-            quantise_block(w, tiles[w])
-            finish(w)
-        if unflipped:
-            flip_and_store(*unflipped.pop())
+                add_sets(nc.gpsimd, h[:, P * s : P * s + P, :], view, SETS * ch + s, 1)
+
+        def ve_block(i, h):
+            group, ch = ve[i]
+            add_sets(nc.vector, h, a_view(group), SETS * ch, SETS)
+
+        quantise_tokens([0], tok0)
+        bank0 = b_pass(0)
+        banks[0] = a_pass(0)
+        b_add(0, bank0)
+        quantise_tokens([1], tok1)
+        bank1 = b_pass(1)
+        a_copy(2)
+        h_first = [work.tile([P, 2 * P, PACK], BF16, align_bytes=64, name="h_first%d" % c) for c in range(2)]
+        add_sets(nc.vector, h_first[0][:], a_view(0), 0, 2)
+        b_add(1, bank1)
+        quantise(0, h_first[0][:])
+        scalar_out(0, 0, 2 * P)
+        add_sets(nc.vector, h_first[1][:], a_view(0), 2, 2)
+        quantise_tokens([2, 3], tok23)
+        bank2 = b_pass(2)
+        bank3 = b_pass(3)
+        b_add(2, bank2)
+        quantise(2 * P, h_first[1][:])
+        scalar_out(0, 2 * P, 2 * P)
+        b_add(3, bank3)
+        pairs = {}
+
+        def start_pair(j):
+            h_pair = work.tile([P, 2 * BLOCK, PACK], BF16, align_bytes=64)
+            pairs[j] = h_pair
+            gp_block(j, h_pair[:, BLOCK : 2 * BLOCK, :])
+
+        start_pair(0)
+        sort_columns(1, 0, high, None, True)
+        a_copy(1)
+        a_copy(7)
+        banks[3] = a_pass(3)
+        banks[4] = a_pass(4)
+
+        def finish(ks):
+            for k in ks:
+                if k >= BLOCKS - DIRECT:
+                    direct_block(k)
+                else:
+                    scalar_out(k)
+
+        singles = {}
+        for j in range(5):
+            ve_block(2 * j + 1, pairs[j][:, 0:BLOCK, :])
+            if j > 0:
+                quantise(BLOCK * 3 * j, singles[j - 1][:])
+                finish([3 * j])
+            if j > 0 and j + 4 < 8:
+                banks[j + 4] = a_pass(j + 4)
+            if j == 0:
+                quantise(BLOCK, pairs[j][:])
+                finish([1, 2])
+                start_pair(1)
+            h_single = work.tile([P, BLOCK, PACK], BF16, align_bytes=64)
+            singles[j] = h_single
+            ve_block(2 * j + 2, h_single[:])
+            if j > 0:
+                quantise(BLOCK * (3 * j + 1), pairs[j][:])
+                finish([3 * j + 1, 3 * j + 2])
+                if j + 1 < 5:
+                    start_pair(j + 1)
+        flush()
+        quantise(BLOCK * 15, singles[4][:])
+        finish([15])

@@ -139,8 +139,8 @@ def tile_simplemodel_pb_t_kernel(
         def b_add(c, bank):
             nc.vector.tensor_tensor(
                 out=b_sb[:, c, :, :, :],
-                in0=bank[:].rearrange("p t (b l) -> p l b t", l=2),
-                in1=corr_bias[:].unsqueeze(1).unsqueeze(1).to_broadcast([P, 2, BATCH, PACK]),
+                in0=corr_bias[:].unsqueeze(1).unsqueeze(1).to_broadcast([P, 2, BATCH, PACK]),
+                in1=bank[:].rearrange("p t (b l) -> p l b t", l=2),
                 op=ADD,
             )
 
@@ -159,8 +159,8 @@ def tile_simplemodel_pb_t_kernel(
             b_view = b_sb[:].rearrange("p c l b t -> p (c l) b t")[:, first_set : first_set + sets, :, :]
             engine.tensor_tensor(
                 out=h.rearrange("p (s b l) t -> p s b l t", l=2, b=BATCH),
-                in0=a_view.unsqueeze(1).to_broadcast(shape),
-                in1=b_view.unsqueeze(3).to_broadcast(shape),
+                in0=b_view.unsqueeze(3).to_broadcast(shape),
+                in1=a_view.unsqueeze(1).to_broadcast(shape),
                 op=ADD,
             )
 
@@ -238,8 +238,8 @@ def tile_simplemodel_pb_t_kernel(
                     )
                 nc.vector.tensor_tensor(
                     out=result[:, :, chunk, :],
-                    in0=acc[:],
-                    in1=cross_row[:].unsqueeze(1).to_broadcast([P, 2, EMBED]),
+                    in0=cross_row[:].unsqueeze(1).to_broadcast([P, 2, EMBED]),
+                    in1=acc[:],
                     op=ADD,
                 )
                 nc.sync.dma_start(out=out_view(group, 2 * ch + chunk, 1), in_=result[:, :, chunk, :])

@@ -21,7 +21,8 @@ CHUNKS = 4
 SETS = 4
 BLOCK = SETS * P
 BLOCKS = 16
-DIRECT = 3
+VE_BLOCKS = 11
+DIRECT = (10, 15)
 HALVES = (0, 0, 1)
 
 FLOPS = 2 * BATCH * TOKENS * TOKENS * 512 * EMBED + 2 * BATCH * TOKENS * PAIRS * 512 * EMBED
@@ -33,7 +34,7 @@ def tile_simplemodel_pb_t_kernel(
     nc = tc.nc
     with tc.tile_pool(name="consts", bufs=1) as consts, tc.tile_pool(name="stage", bufs=3) as stage, tc.tile_pool(
         name="work", bufs=3
-    ) as work, tc.tile_pool(name="results", bufs=6) as results, tc.psum_pool(
+    ) as work, tc.tile_pool(name="results", bufs=6) as results, tc.tile_pool(name="half", bufs=1) as half_pool, tc.psum_pool(
         name="psum_acc", bufs=3
     ) as psum_acc, tc.psum_pool(
         name="psum_flips", bufs=2
@@ -245,11 +246,9 @@ def tile_simplemodel_pb_t_kernel(
                 nc.sync.dma_start(out=out_view(group, 2 * ch + chunk, 1), in_=result[:, :, chunk, :])
 
         VE_GROUPS = [0, 3, 4, 5, 6, 7]
-        ve = [(g, ch) for g in VE_GROUPS for ch in range(2)][0:11]
+        ve = [(g, ch) for g in VE_GROUPS for ch in range(2)][0:VE_BLOCKS]
         gp = [(2, 0), (2, 1), (1, 0), (1, 1), (7, 1)]
-        block_of = [ve[0]]
-        for j in range(5):
-            block_of += [ve[2 * j + 1], gp[j], ve[2 * j + 2]]
+        block_of = ve + gp
 
         def sort_columns(variant, h, rows, cols, dup):
             view = w1_raw[rows, h, :].rearrange("p (q t) -> p t q", t=PACK)
@@ -292,15 +291,11 @@ def tile_simplemodel_pb_t_kernel(
             flush()
             unflipped.append((k, first, rows, out_t))
 
-        def gp_block(j, h):
-            group, ch = gp[j]
-            view = a_sb[:, group, :, :].rearrange("p (b l) t -> p b l t", l=2)
-            for s in range(SETS):
-                add_sets(nc.gpsimd, h[:, P * s : P * s + P, :], view, SETS * ch + s, 1)
-
-        def ve_block(i, h):
-            group, ch = ve[i]
-            add_sets(nc.vector, h, a_view(group), SETS * ch, SETS)
+        def finish(k):
+            if k in DIRECT:
+                direct_block(k)
+            else:
+                scalar_out(k)
 
         quantise_tokens([0], tok0)
         bank0 = b_pass(0)
@@ -309,60 +304,51 @@ def tile_simplemodel_pb_t_kernel(
         quantise_tokens([1], tok1)
         bank1 = b_pass(1)
         a_copy(2)
-        h_first = [work.tile([P, 2 * P, PACK], BF16, align_bytes=64, name="h_first%d" % c) for c in range(2)]
-        add_sets(nc.vector, h_first[0][:], a_view(0), 0, 2)
+        h_half = half_pool.tile([P, 2 * P, PACK], BF16, align_bytes=64)
+        add_sets(nc.vector, h_half[:], a_view(0), 0, 2)
         b_add(1, bank1)
-        quantise(0, h_first[0][:])
+        quantise(0, h_half[:])
         scalar_out(0, 0, 2 * P)
-        add_sets(nc.vector, h_first[1][:], a_view(0), 2, 2)
+        h_half = half_pool.tile([P, 2 * P, PACK], BF16, align_bytes=64)
+        add_sets(nc.vector, h_half[:], a_view(0), 2, 2)
         quantise_tokens([2, 3], tok23)
         bank2 = b_pass(2)
         bank3 = b_pass(3)
         b_add(2, bank2)
-        quantise(2 * P, h_first[1][:])
+        sort_columns(1, 0, high, None, True)
+        quantise(2 * P, h_half[:])
         scalar_out(0, 2 * P, 2 * P)
         b_add(3, bank3)
-        pairs = {}
 
-        def start_pair(j):
-            h_pair = work.tile([P, 2 * BLOCK, PACK], BF16, align_bytes=64)
-            pairs[j] = h_pair
-            gp_block(j, h_pair[:, BLOCK : 2 * BLOCK, :])
+        def gp_half(j):
+            group, ch = gp[j // 2]
+            h_half = half_pool.tile([P, 2 * P, PACK], BF16, align_bytes=64)
+            view = a_sb[:, group, :, :].rearrange("p (b l) t -> p b l t", l=2)
+            add_sets(nc.gpsimd, h_half[:], view, SETS * ch + 2 * (j % 2), 2)
+            return h_half
 
-        start_pair(0)
-        sort_columns(1, 0, high, None, True)
+        gp_tile = gp_half(0)
         a_copy(1)
         a_copy(7)
         banks[3] = a_pass(3)
         banks[4] = a_pass(4)
-
-        def finish(ks):
-            for k in ks:
-                if k >= BLOCKS - DIRECT:
-                    direct_block(k)
-                else:
-                    scalar_out(k)
-
-        singles = {}
-        for j in range(5):
-            ve_block(2 * j + 1, pairs[j][:, 0:BLOCK, :])
-            if j > 0:
-                quantise(BLOCK * 3 * j, singles[j - 1][:])
-                finish([3 * j])
-            if j > 0 and j + 4 < 8:
-                banks[j + 4] = a_pass(j + 4)
-            if j == 0:
-                quantise(BLOCK, pairs[j][:])
-                finish([1, 2])
-                start_pair(1)
-            h_single = work.tile([P, BLOCK, PACK], BF16, align_bytes=64)
-            singles[j] = h_single
-            ve_block(2 * j + 2, h_single[:])
-            if j > 0:
-                quantise(BLOCK * (3 * j + 1), pairs[j][:])
-                finish([3 * j + 1, 3 * j + 2])
-                if j + 1 < 5:
-                    start_pair(j + 1)
+        for i in range(1, VE_BLOCKS):
+            group, ch = ve[i]
+            h_ve = work.tile([P, BLOCK, PACK], BF16, align_bytes=64)
+            add_sets(nc.vector, h_ve[:], a_view(group), SETS * ch, SETS)
+            j = i - 1
+            k_gp = VE_BLOCKS + j // 2
+            quantise(BLOCK * k_gp + 2 * P * (j % 2), gp_tile[:])
+            if j % 2 == 1 and k_gp not in DIRECT:
+                finish(k_gp)
+            quantise(BLOCK * i, h_ve[:])
+            if j % 2 == 1 and k_gp in DIRECT:
+                finish(k_gp)
+            finish(i)
+            if i + 1 < VE_BLOCKS:
+                gp_tile = gp_half(i)
+            if ch == 0 and i > 3 and group < 7:
+                banks[group + 1] = a_pass(group + 1)
+            if i == VE_BLOCKS - 2:
+                flush()
         flush()
-        quantise(BLOCK * 15, singles[4][:])
-        finish([15])

@@ -23,7 +23,7 @@ BLOCK = SETS * P
 BLOCKS = 16
 VE_BLOCKS = 11
 DIRECT = (10, 15)
-HALVES = (0, 0, 1)
+HALVES = (0, 1)
 
 FLOPS = 2 * BATCH * TOKENS * TOKENS * 512 * EMBED + 2 * BATCH * TOKENS * PAIRS * 512 * EMBED
 

@@ -22,7 +22,6 @@ SETS = 4
 BLOCK = SETS * P
 BLOCKS = 16
 VE_BLOCKS = 11
-DIRECT = (10, 15)
 HALVES = (0, 1)
 
 FLOPS = 2 * BATCH * TOKENS * TOKENS * 512 * EMBED + 2 * BATCH * TOKENS * PAIRS * 512 * EMBED
@@ -39,8 +38,10 @@ def tile_simplemodel_pb_t_kernel(
     ) as psum_acc, tc.psum_pool(
         name="psum_flips", bufs=2
     ) as psum_flips, tc.psum_pool(
-        name="psum_a", bufs=3
-    ) as psum_a, tc.manual_schedule():
+        name="psum_a", bufs=2
+    ) as psum_a, tc.psum_pool(
+        name="psum_direct", bufs=1
+    ) as psum_direct, tc.manual_schedule():
         tok_sb = consts.tile([P, CHUNKS, 2 * EMBED], BF16)
         tok_rows = tok.rearrange("b (m j) e -> (b m) (j e)", j=2).rearrange("(p c) e -> p c e", c=CHUNKS)
         w1_raw = consts.tile([P, 2, EMBED], I32, align_bytes=64)
@@ -50,20 +51,20 @@ def tile_simplemodel_pb_t_kernel(
         w2_words = consts.tile([P, EMBED], I32, align_bytes=64)
         w2_scales = consts.tile([P, EMBED], U8, align_bytes=64)
         warm = consts.tile([P, 2], F32)
-        nc.vector.memset(s1_raw[:].bitcast(I32), 0)
+        nc.gpsimd.memset(s1_raw[:].bitcast(I32), 0)
         nc.vector.memset(warm[:], 0.0)
         nc.vector.memset(w1_words[:], 0)
         nc.vector.memset(w2_scales[:].bitcast(I32), 0)
 
-        w1_halves = corr_w_words[0].rearrange("p n t -> p (n t)").bitcast(I32).rearrange("(h p) n -> p h n", h=2)
-        for j in range(2):
-            nc.sync.dma_start(out=w1_raw[HALF * j : HALF * j + HALF, :, :], in_=w1_halves)
-        nc.sync.dma_start(out=tok_sb[:, 0, :], in_=tok_rows[:, 0, :])
         s1_rows = corr_w_scales[0].bitcast(I32).rearrange("(h q r) n -> q r h n", h=2, q=2)
         for j in range(2):
             for q in range(2):
                 first = HALF * j + 32 * q
                 nc.sync.dma_start(out=s1_raw[first : first + 4, :, :].bitcast(I32), in_=s1_rows[q])
+        nc.sync.dma_start(out=tok_sb[:, 0, :], in_=tok_rows[:, 0, :])
+        w1_halves = corr_w_words[0].rearrange("p n t -> p (n t)").bitcast(I32).rearrange("(h p) n -> p h n", h=2)
+        for j in range(2):
+            nc.sync.dma_start(out=w1_raw[HALF * j : HALF * j + HALF, :, :], in_=w1_halves)
         nc.sync.dma_start(out=tok_sb[:, 1, :], in_=tok_rows[:, 1, :])
         nc.sync.dma_start(out=tok_sb[:, 2:4, :], in_=tok_rows[:, 2:4, :])
         nc.sync.dma_start(out=w2_words[:], in_=cross_w_words[0].rearrange("p n t -> p (n t)").bitcast(I32))
@@ -221,29 +222,31 @@ def tile_simplemodel_pb_t_kernel(
                 out=out_view(group, c0, chunks), in_=result[:, :, 0:chunks, :].rearrange("p l c n -> p l (c n)")
             )
 
-        def direct_block(k):
-            group, ch = block_of[k]
-            result = results.tile([P, 2, 2, EMBED], F32)
-            for chunk in range(2):
-                acc = psum_a.tile([P, 2, EMBED], F32, tag="a")
-                for l in range(2):
-                    first = P * (2 * chunk + l)
-                    nc.tensor.matmul_mx(
-                        out=acc[:, l, :],
-                        lhsT=h_codes[:, k, first : first + P].bitcast(FP8X4),
-                        lhsT_scale=h_scales[:, k, first : first + P],
-                        rhs=w2_words[:].bitcast(FP8X4),
-                        rhs_scale=w2_scales[:],
-                        start=True,
-                        stop=True,
-                    )
-                nc.vector.tensor_tensor(
-                    out=result[:, :, chunk, :],
-                    in0=cross_row[:].unsqueeze(1).to_broadcast([P, 2, EMBED]),
-                    in1=acc[:],
-                    op=ADD,
+        def direct_matmul(k, chunk):
+            acc = psum_direct.tile([P, 2, EMBED], F32, tag="direct")
+            for l in range(2):
+                first = P * (2 * chunk + l)
+                nc.tensor.matmul_mx(
+                    out=acc[:, l, :],
+                    lhsT=h_codes[:, k, first : first + P].bitcast(FP8X4),
+                    lhsT_scale=h_scales[:, k, first : first + P],
+                    rhs=w2_words[:].bitcast(FP8X4),
+                    rhs_scale=w2_scales[:],
+                    start=True,
+                    stop=True,
                 )
-                nc.sync.dma_start(out=out_view(group, 2 * ch + chunk, 1), in_=result[:, :, chunk, :])
+            return acc
+
+        def direct_store(k, chunk, acc):
+            group, ch = block_of[k]
+            result = results.tile([P, 2, EMBED], F32, name="direct_result")
+            nc.vector.tensor_tensor(
+                out=result[:],
+                in0=cross_row[:].unsqueeze(1).to_broadcast([P, 2, EMBED]),
+                in1=acc[:],
+                op=ADD,
+            )
+            nc.sync.dma_start(out=out_view(group, 2 * ch + chunk, 1), in_=result[:])
 
         VE_GROUPS = [0, 3, 4, 5, 6, 7]
         ve = [(g, ch) for g in VE_GROUPS for ch in range(2)][0:VE_BLOCKS]
@@ -291,12 +294,6 @@ def tile_simplemodel_pb_t_kernel(
             flush()
             unflipped.append((k, first, rows, out_t))
 
-        def finish(k):
-            if k in DIRECT:
-                direct_block(k)
-            else:
-                scalar_out(k)
-
         quantise_tokens([0], tok0)
         bank0 = b_pass(0)
         banks[0] = a_pass(0)
@@ -331,24 +328,26 @@ def tile_simplemodel_pb_t_kernel(
         a_copy(1)
         a_copy(7)
         banks[3] = a_pass(3)
-        banks[4] = a_pass(4)
+        following = {0: 4, 3: 5, 4: 6, 5: 7, 6: None}
+        waiting = None
         for i in range(1, VE_BLOCKS):
             group, ch = ve[i]
             h_ve = work.tile([P, BLOCK, PACK], BF16, align_bytes=64)
             add_sets(nc.vector, h_ve[:], a_view(group), SETS * ch, SETS)
+            if waiting is not None:
+                direct_store(*waiting)
             j = i - 1
             k_gp = VE_BLOCKS + j // 2
             quantise(BLOCK * k_gp + 2 * P * (j % 2), gp_tile[:])
-            if j % 2 == 1 and k_gp not in DIRECT:
-                finish(k_gp)
+            waiting = (k_gp, j % 2, direct_matmul(k_gp, j % 2))
             quantise(BLOCK * i, h_ve[:])
-            if j % 2 == 1 and k_gp in DIRECT:
-                finish(k_gp)
-            finish(i)
             if i + 1 < VE_BLOCKS:
                 gp_tile = gp_half(i)
-            if ch == 0 and i > 3 and group < 7:
-                banks[group + 1] = a_pass(group + 1)
-            if i == VE_BLOCKS - 2:
+                scalar_out(i)
+                if ch == 1 and following[group] is not None:
+                    banks[following[group]] = a_pass(following[group])
+            else:
                 flush()
-        flush()
+                direct_store(*waiting)
+                for chunk in range(2):
+                    direct_store(i, chunk, direct_matmul(i, chunk))

@@ -23,6 +23,7 @@ BLOCK = SETS * P
 BLOCKS = 16
 VE_BLOCKS = 11
 HALVES = (0, 1)
+DIRECT = (14, 15)
 
 FLOPS = 2 * BATCH * TOKENS * TOKENS * 512 * EMBED + 2 * BATCH * TOKENS * PAIRS * 512 * EMBED
 
@@ -51,38 +52,37 @@ def tile_simplemodel_pb_t_kernel(
         w2_words = consts.tile([P, EMBED], I32, align_bytes=64)
         w2_scales = consts.tile([P, EMBED], U8, align_bytes=64)
         warm = consts.tile([P, 2], F32)
-        nc.gpsimd.memset(s1_raw[:].bitcast(I32), 0)
+        nc.vector.memset(s1_raw[:].bitcast(I32), 0)
         nc.vector.memset(warm[:], 0.0)
+        nc.scalar.activation(out=warm[:, 1:2], in_=warm[:, 0:1], func=IDENTITY, bias=0.0, scale=1.0)
         nc.vector.memset(w1_words[:], 0)
         nc.vector.memset(w2_scales[:].bitcast(I32), 0)
 
+        nc.sync.dma_start(out=tok_sb[:, 0:2, :], in_=tok_rows[:, 0:2, :])
+        w1_halves = corr_w_words[0].rearrange("p n t -> p (n t)").bitcast(I32).rearrange("(h p) n -> p h n", h=2)
+        for j in range(2):
+            nc.sync.dma_start(out=w1_raw[HALF * j : HALF * j + HALF, :, :], in_=w1_halves)
         s1_rows = corr_w_scales[0].bitcast(I32).rearrange("(h q r) n -> q r h n", h=2, q=2)
         for j in range(2):
             for q in range(2):
                 first = HALF * j + 32 * q
                 nc.sync.dma_start(out=s1_raw[first : first + 4, :, :].bitcast(I32), in_=s1_rows[q])
-        nc.sync.dma_start(out=tok_sb[:, 0, :], in_=tok_rows[:, 0, :])
-        w1_halves = corr_w_words[0].rearrange("p n t -> p (n t)").bitcast(I32).rearrange("(h p) n -> p h n", h=2)
-        for j in range(2):
-            nc.sync.dma_start(out=w1_raw[HALF * j : HALF * j + HALF, :, :], in_=w1_halves)
-        nc.sync.dma_start(out=tok_sb[:, 1, :], in_=tok_rows[:, 1, :])
-        nc.sync.dma_start(out=tok_sb[:, 2:4, :], in_=tok_rows[:, 2:4, :])
-        nc.sync.dma_start(out=w2_words[:], in_=cross_w_words[0].rearrange("p n t -> p (n t)").bitcast(I32))
-        s2_rows = cross_w_scales[0].bitcast(I32)
-        for q in range(4):
-            nc.sync.dma_start(out=w2_scales[32 * q : 32 * q + 4, :].bitcast(I32), in_=s2_rows[4 * q : 4 * q + 4, :])
-
         corr_bias = consts.tile([P, PACK], BF16)
         for half in range(2):
             nc.scalar.dma_start(
                 out=corr_bias[HALF * half : HALF * half + HALF, :], in_=corr_b.rearrange("(q t) -> q t", t=PACK)
             )
+        nc.sync.dma_start(out=tok_sb[:, 2:4, :], in_=tok_rows[:, 2:4, :])
         cross_bias = consts.tile([P, 2], BF16)
         with nc.allow_non_contiguous_dma(reason="256 bias values, one to a partition"):
-            nc.scalar.dma_start(out=cross_bias[:], in_=cross_b.rearrange("(c m) -> m c", c=2))
+            nc.sync.dma_start(out=cross_bias[:], in_=cross_b.rearrange("(c m) -> m c", c=2))
+        nc.sync.dma_start(out=w2_words[:], in_=cross_w_words[0].rearrange("p n t -> p (n t)").bitcast(I32))
+        s2_rows = cross_w_scales[0].bitcast(I32)
+        for q in range(4):
+            nc.sync.dma_start(out=w2_scales[32 * q : 32 * q + 4, :].bitcast(I32), in_=s2_rows[4 * q : 4 * q + 4, :])
+
         cross_row = consts.tile([P, EMBED], BF16)
         nc.sync.dma_start(out=cross_row[:], in_=cross_b.partition_broadcast(P))
-        nc.scalar.activation(out=warm[:, 1:2], in_=warm[:, 0:1], func=IDENTITY, bias=0.0, scale=1.0)
 
         ident = consts.tile([P, P], F32)
         make_identity(nc, ident[:])
@@ -336,13 +336,18 @@ def tile_simplemodel_pb_t_kernel(
             add_sets(nc.vector, h_ve[:], a_view(group), SETS * ch, SETS)
             if waiting is not None:
                 direct_store(*waiting)
+                waiting = None
             j = i - 1
             k_gp = VE_BLOCKS + j // 2
             quantise(BLOCK * k_gp + 2 * P * (j % 2), gp_tile[:])
-            waiting = (k_gp, j % 2, direct_matmul(k_gp, j % 2))
             quantise(BLOCK * i, h_ve[:])
             if i + 1 < VE_BLOCKS:
                 gp_tile = gp_half(i)
+            if k_gp in DIRECT:
+                waiting = (k_gp, j % 2, direct_matmul(k_gp, j % 2))
+            elif j % 2 == 1:
+                scalar_out(k_gp)
+            if i + 1 < VE_BLOCKS:
                 scalar_out(i)
                 if ch == 1 and following[group] is not None:
                     banks[following[group]] = a_pass(following[group])

@@ -23,7 +23,7 @@ BLOCK = SETS * P
 BLOCKS = 16
 VE_BLOCKS = 11
 HALVES = (0, 1)
-DIRECT = (14, 15)
+DIRECT_HALVES = 3
 
 FLOPS = 2 * BATCH * TOKENS * TOKENS * 512 * EMBED + 2 * BATCH * TOKENS * PAIRS * 512 * EMBED
 
@@ -67,12 +67,12 @@ def tile_simplemodel_pb_t_kernel(
             for q in range(2):
                 first = HALF * j + 32 * q
                 nc.sync.dma_start(out=s1_raw[first : first + 4, :, :].bitcast(I32), in_=s1_rows[q])
+        nc.sync.dma_start(out=tok_sb[:, 2:4, :], in_=tok_rows[:, 2:4, :])
         corr_bias = consts.tile([P, PACK], BF16)
         for half in range(2):
             nc.scalar.dma_start(
                 out=corr_bias[HALF * half : HALF * half + HALF, :], in_=corr_b.rearrange("(q t) -> q t", t=PACK)
             )
-        nc.sync.dma_start(out=tok_sb[:, 2:4, :], in_=tok_rows[:, 2:4, :])
         cross_bias = consts.tile([P, 2], BF16)
         with nc.allow_non_contiguous_dma(reason="256 bias values, one to a partition"):
             nc.sync.dma_start(out=cross_bias[:], in_=cross_b.rearrange("(c m) -> m c", c=2))
@@ -145,6 +145,47 @@ def tile_simplemodel_pb_t_kernel(
                 in1=bank[:].rearrange("p t (b l) -> p l b t", l=2),
                 op=ADD,
             )
+
+        def spread_corr_bias():
+            corr_f32 = consts.tile([P, PACK], F32)
+            nc.scalar.copy(out=corr_f32[:], in_=corr_bias[:])
+            bank = psum_flips.tile([P, PACK, P], F32, tag="flips")
+            for t in range(PACK):
+                nc.tensor.transpose(
+                    out=bank[:, t, :], in_=corr_f32[:, t : t + 1].to_broadcast([P, P]), identity=ident[:]
+                )
+            corr_rows = consts.tile([P, PACK, P], F32)
+            nc.scalar.copy(out=corr_rows[:], in_=bank[:])
+            return corr_rows
+
+        def b_rows(c):
+            bank = psum_acc.tile([P, PACK, P], F32, tag="acc")
+            nc.tensor.matmul_mx(
+                out=bank[:].rearrange("p t n -> p (t n)"),
+                lhsT=x_codes[:, P * c : P * c + P].bitcast(FP8X4),
+                lhsT_scale=x_scales[:, P * c : P * c + P],
+                rhs=w1_words[:, 2, :, :].rearrange("p t n -> p (t n)").bitcast(FP8X4),
+                rhs_scale=s1[:, 1, :, :].rearrange("p t n -> p (t n)"),
+                start=True,
+                stop=True,
+            )
+            rows = stage.tile([P, PACK, P], F32, name="rows")
+            nc.scalar.copy(out=rows[:], in_=bank[:])
+            return rows
+
+        def b_turn(c, rows, corr_rows):
+            bank = psum_acc.tile([P, PACK, P], F32, tag="acc")
+            for t in range(PACK):
+                for term, lhsT in enumerate((rows, corr_rows)):
+                    nc.tensor.matmul(
+                        out=bank[:, t, :],
+                        lhsT=lhsT[:, t, :],
+                        rhs=ident[:],
+                        is_transpose=True,
+                        start=term == 0,
+                        stop=term == 1,
+                    )
+            nc.scalar.copy(out=b_sb[:, c, :, :, :], in_=bank[:].rearrange("p t (b l) -> p l b t", l=2))
 
         def a_pass(group):
             bank = psum_a.tile([P, PACK, P], F32, tag="a")
@@ -250,6 +291,7 @@ def tile_simplemodel_pb_t_kernel(
 
         VE_GROUPS = [0, 3, 4, 5, 6, 7]
         ve = [(g, ch) for g in VE_GROUPS for ch in range(2)][0:VE_BLOCKS]
+        ve[1], ve[2] = ve[2], ve[1]
         gp = [(2, 0), (2, 1), (1, 0), (1, 1), (7, 1)]
         block_of = ve + gp
 
@@ -297,25 +339,29 @@ def tile_simplemodel_pb_t_kernel(
         quantise_tokens([0], tok0)
         bank0 = b_pass(0)
         banks[0] = a_pass(0)
-        b_add(0, bank0)
         quantise_tokens([1], tok1)
+        sort_columns(1, 0, high, None, True)
+        b_add(0, bank0)
+        quantise_tokens([2, 3], tok23)
         bank1 = b_pass(1)
+        banks[3] = a_pass(3)
         a_copy(2)
-        h_half = half_pool.tile([P, 2 * P, PACK], BF16, align_bytes=64)
+        corr_rows = spread_corr_bias()
+        rows2 = b_rows(2)
+        rows3 = b_rows(3)
+        h_half = half_pool.tile([P, 2 * P, PACK], BF16, align_bytes=64, tag="half")
         add_sets(nc.vector, h_half[:], a_view(0), 0, 2)
         b_add(1, bank1)
+        b_turn(2, rows2, corr_rows)
+        b_turn(3, rows3, corr_rows)
         quantise(0, h_half[:])
         scalar_out(0, 0, 2 * P)
-        h_half = half_pool.tile([P, 2 * P, PACK], BF16, align_bytes=64)
+        h_half = half_pool.tile([P, 2 * P, PACK], BF16, align_bytes=64, tag="half")
         add_sets(nc.vector, h_half[:], a_view(0), 2, 2)
-        quantise_tokens([2, 3], tok23)
-        bank2 = b_pass(2)
-        bank3 = b_pass(3)
-        b_add(2, bank2)
-        sort_columns(1, 0, high, None, True)
+        a_copy(7)
+        a_copy(1)
         quantise(2 * P, h_half[:])
         scalar_out(0, 2 * P, 2 * P)
-        b_add(3, bank3)
 
         def gp_half(j):
             group, ch = gp[j // 2]
@@ -325,9 +371,6 @@ def tile_simplemodel_pb_t_kernel(
             return h_half
 
         gp_tile = gp_half(0)
-        a_copy(1)
-        a_copy(7)
-        banks[3] = a_pass(3)
         following = {0: 4, 3: 5, 4: 6, 5: 7, 6: None}
         waiting = None
         for i in range(1, VE_BLOCKS):
@@ -343,14 +386,16 @@ def tile_simplemodel_pb_t_kernel(
             quantise(BLOCK * i, h_ve[:])
             if i + 1 < VE_BLOCKS:
                 gp_tile = gp_half(i)
-            if k_gp in DIRECT:
+                if ch == 1 and following[group] is not None:
+                    banks[following[group]] = a_pass(following[group])
+            if j >= 10 - DIRECT_HALVES:
                 waiting = (k_gp, j % 2, direct_matmul(k_gp, j % 2))
+                if j == 10 - DIRECT_HALVES and j % 2 == 1:
+                    scalar_out(k_gp, 0, 2 * P)
             elif j % 2 == 1:
                 scalar_out(k_gp)
             if i + 1 < VE_BLOCKS:
                 scalar_out(i)
-                if ch == 1 and following[group] is not None:
-                    banks[following[group]] = a_pass(following[group])
             else:
                 flush()
                 direct_store(*waiting)

import concourse.mybir as mybir
from concourse.masks import make_identity

F32 = mybir.dt.float32
BF16 = mybir.dt.bfloat16
I32 = mybir.dt.int32
U32 = mybir.dt.uint32
U8 = mybir.dt.uint8
FP8X4 = mybir.dt.float8_e4m3fn_x4
IDENTITY = mybir.ActivationFunctionType.Identity
ADD = mybir.AluOpType.add

P = 128
HALF = 64
PACK = 4
BATCH = 64
TOKENS = 16
PAIRS = 8
EMBED = 256
CHUNKS = 4
SETS = 4
BLOCK = SETS * P
BLOCKS = 16
VE_BLOCKS = 11
HALVES = (0, 1)
DIRECT_HALVES = 3

FLOPS = 2 * BATCH * TOKENS * TOKENS * 512 * EMBED + 2 * BATCH * TOKENS * PAIRS * 512 * EMBED


def tile_simplemodel_pb_t_kernel(
    tc, tok, corr_w_words, corr_w_scales, corr_b, cross_w_words, cross_w_scales, cross_b, out
):
    nc = tc.nc
    with tc.tile_pool(name="consts", bufs=1) as consts, tc.tile_pool(name="stage", bufs=3) as stage, tc.tile_pool(
        name="work", bufs=3
    ) as work, tc.tile_pool(name="results", bufs=6) as results, tc.tile_pool(name="half", bufs=1) as half_pool, tc.psum_pool(
        name="psum_acc", bufs=3
    ) as psum_acc, tc.psum_pool(
        name="psum_flips", bufs=2
    ) as psum_flips, tc.psum_pool(
        name="psum_a", bufs=2
    ) as psum_a, tc.psum_pool(
        name="psum_direct", bufs=1
    ) as psum_direct, tc.manual_schedule():
        tok_sb = consts.tile([P, CHUNKS, 2 * EMBED], BF16)
        tok_rows = tok.rearrange("b (m j) e -> (b m) (j e)", j=2).rearrange("(p c) e -> p c e", c=CHUNKS)
        w1_raw = consts.tile([P, 2, EMBED], I32, align_bytes=64)
        s1_raw = consts.tile([P, 2, EMBED], U8, align_bytes=64)
        w1_words = consts.tile([P, 3, PACK, P], I32, align_bytes=64)
        s1 = consts.tile([P, 2, PACK, P], U8, align_bytes=64)
        w2_words = consts.tile([P, EMBED], I32, align_bytes=64)
        w2_scales = consts.tile([P, EMBED], U8, align_bytes=64)
        warm = consts.tile([P, 2], F32)
        nc.vector.memset(s1_raw[:].bitcast(I32), 0)
        nc.vector.memset(warm[:], 0.0)
        nc.scalar.activation(out=warm[:, 1:2], in_=warm[:, 0:1], func=IDENTITY, bias=0.0, scale=1.0)
        nc.vector.memset(w1_words[:], 0)
        nc.vector.memset(w2_scales[:].bitcast(I32), 0)

        nc.sync.dma_start(out=tok_sb[:, 0:2, :], in_=tok_rows[:, 0:2, :])
        w1_halves = corr_w_words[0].rearrange("p n t -> p (n t)").bitcast(I32).rearrange("(h p) n -> p h n", h=2)
        for j in range(2):
            nc.sync.dma_start(out=w1_raw[HALF * j : HALF * j + HALF, :, :], in_=w1_halves)
        s1_rows = corr_w_scales[0].bitcast(I32).rearrange("(h q r) n -> q r h n", h=2, q=2)
        for j in range(2):
            for q in range(2):
                first = HALF * j + 32 * q
                nc.sync.dma_start(out=s1_raw[first : first + 4, :, :].bitcast(I32), in_=s1_rows[q])
        nc.sync.dma_start(out=tok_sb[:, 2:4, :], in_=tok_rows[:, 2:4, :])
        corr_bias = consts.tile([P, PACK], BF16)
        for half in range(2):
            nc.scalar.dma_start(
                out=corr_bias[HALF * half : HALF * half + HALF, :], in_=corr_b.rearrange("(q t) -> q t", t=PACK)
            )
        cross_bias = consts.tile([P, 2], BF16)
        with nc.allow_non_contiguous_dma(reason="256 bias values, one to a partition"):
            nc.sync.dma_start(out=cross_bias[:], in_=cross_b.rearrange("(c m) -> m c", c=2))
        nc.sync.dma_start(out=w2_words[:], in_=cross_w_words[0].rearrange("p n t -> p (n t)").bitcast(I32))
        s2_rows = cross_w_scales[0].bitcast(I32)
        for q in range(4):
            nc.sync.dma_start(out=w2_scales[32 * q : 32 * q + 4, :].bitcast(I32), in_=s2_rows[4 * q : 4 * q + 4, :])

        cross_row = consts.tile([P, EMBED], BF16)
        nc.sync.dma_start(out=cross_row[:], in_=cross_b.partition_broadcast(P))

        ident = consts.tile([P, P], F32)
        make_identity(nc, ident[:])

        x_codes = consts.tile([P, CHUNKS * P], U32, align_bytes=64)
        x_scales = consts.tile([P, CHUNKS * P], U8, align_bytes=64)
        b_sb = consts.tile([P, CHUNKS, 2, BATCH, PACK], F32)
        a_sb = consts.tile([P, 8, P, PACK], F32)
        h_codes = consts.tile([P, BLOCKS, BLOCK], U32, align_bytes=64)
        h_scales = consts.tile([P, BLOCKS, BLOCK], U8, align_bytes=64)
        out_rows = out.rearrange("b (l r) m n -> (b l) r (m n)", l=2)

        def turn_tokens(chunks):
            n = len(chunks)
            tok_t = psum_flips.tile([P, 2, 2, P], F32, tag="flips")
            for k in range(n):
                words = tok_sb[:, chunks[k], :].bitcast(F32)
                for u in range(2):
                    nc.tensor.transpose(out=tok_t[:, k, u, :], in_=words[:, u : EMBED : 2], identity=ident[:])
            grouped = stage.tile([P, 2 * P, PACK], BF16, align_bytes=64)
            nc.scalar.copy(
                out=grouped[:, 0 : n * P, :]
                .rearrange("p n t -> p (n t)")
                .bitcast(F32)
                .rearrange("p (k n u) -> p k n u", k=n, u=2),
                in_=tok_t[:, 0:n, :, :].rearrange("p k u n -> p k n u"),
            )
            return grouped

        def quantise_tokens(chunks, grouped):
            cols = slice(P * chunks[0], P * chunks[0] + P * len(chunks))
            nc.vector.quantize_mx(
                out=x_codes[:, cols].bitcast(FP8X4),
                scales=x_scales[:, cols],
                in_=grouped[:, 0 : P * len(chunks), :].rearrange("p n t -> p (n t)"),
            )

        def first_pass(bank, variant, c):
            scales = 1 if variant == 2 else 0
            for t in range(PACK):
                nc.tensor.matmul_mx(
                    out=bank[:, t, :],
                    lhsT=w1_words[:, variant, t, :].bitcast(FP8X4),
                    lhsT_scale=s1[:, scales, t, :],
                    rhs=x_codes[:, P * c : P * c + P].bitcast(FP8X4),
                    rhs_scale=x_scales[:, P * c : P * c + P],
                    start=True,
                    stop=True,
                )

        def b_pass(c):
            bank = psum_acc.tile([P, PACK, P], F32, tag="acc")
            first_pass(bank, 2, c)
            return bank

        def b_add(c, bank):
            nc.vector.tensor_tensor(
                out=b_sb[:, c, :, :, :],
                in0=corr_bias[:].unsqueeze(1).unsqueeze(1).to_broadcast([P, 2, BATCH, PACK]),
                in1=bank[:].rearrange("p t (b l) -> p l b t", l=2),
                op=ADD,
            )

        def spread_corr_bias():
            corr_f32 = consts.tile([P, PACK], F32)
            nc.scalar.copy(out=corr_f32[:], in_=corr_bias[:])
            bank = psum_flips.tile([P, PACK, P], F32, tag="flips")
            for t in range(PACK):
                nc.tensor.transpose(
                    out=bank[:, t, :], in_=corr_f32[:, t : t + 1].to_broadcast([P, P]), identity=ident[:]
                )
            corr_rows = consts.tile([P, PACK, P], F32)
            nc.scalar.copy(out=corr_rows[:], in_=bank[:])
            return corr_rows

        def b_rows(c):
            bank = psum_acc.tile([P, PACK, P], F32, tag="acc")
            nc.tensor.matmul_mx(
                out=bank[:].rearrange("p t n -> p (t n)"),
                lhsT=x_codes[:, P * c : P * c + P].bitcast(FP8X4),
                lhsT_scale=x_scales[:, P * c : P * c + P],
                rhs=w1_words[:, 2, :, :].rearrange("p t n -> p (t n)").bitcast(FP8X4),
                rhs_scale=s1[:, 1, :, :].rearrange("p t n -> p (t n)"),
                start=True,
                stop=True,
            )
            rows = stage.tile([P, PACK, P], F32, name="rows")
            nc.scalar.copy(out=rows[:], in_=bank[:])
            return rows

        def b_turn(c, rows, corr_rows):
            bank = psum_acc.tile([P, PACK, P], F32, tag="acc")
            for t in range(PACK):
                for term, lhsT in enumerate((rows, corr_rows)):
                    nc.tensor.matmul(
                        out=bank[:, t, :],
                        lhsT=lhsT[:, t, :],
                        rhs=ident[:],
                        is_transpose=True,
                        start=term == 0,
                        stop=term == 1,
                    )
            nc.scalar.copy(out=b_sb[:, c, :, :, :], in_=bank[:].rearrange("p t (b l) -> p l b t", l=2))

        def a_pass(group):
            bank = psum_a.tile([P, PACK, P], F32, tag="a")
            first_pass(bank, group % 2, group // 2)
            return bank

        def a_copy(group):
            bank = psum_acc.tile([P, PACK, P], F32, tag="acc")
            first_pass(bank, group % 2, group // 2)
            nc.scalar.copy(out=a_sb[:, group, :, :], in_=bank[:].rearrange("p t n -> p n t"))

        def add_sets(engine, h, a_view, first_set, sets):
            shape = [P, sets, BATCH, 2, PACK]
            b_view = b_sb[:].rearrange("p c l b t -> p (c l) b t")[:, first_set : first_set + sets, :, :]
            engine.tensor_tensor(
                out=h.rearrange("p (s b l) t -> p s b l t", l=2, b=BATCH),
                in0=b_view.unsqueeze(3).to_broadcast(shape),
                in1=a_view.unsqueeze(1).to_broadcast(shape),
                op=ADD,
            )

        def quantise(first, h):
            flat_codes = h_codes[:].rearrange("p k n -> p (k n)")
            flat_scales = h_scales[:].rearrange("p k n -> p (k n)")
            n = h.shape[1]
            nc.vector.quantize_mx(
                out=flat_codes[:, first : first + n].bitcast(FP8X4),
                scales=flat_scales[:, first : first + n],
                in_=h.rearrange("p r t -> p (r t)"),
            )

        def out_view(group, c, chunks):
            r = 2 * (group // 2) + group % 2
            view = out_rows[:, r, :].rearrange("p (l c n) -> p l c n", l=2, c=CHUNKS)
            return view[:, :, c : c + chunks, :].rearrange("p l c n -> p l (c n)")

        def second_matmul(k, first, rows):
            out_t = work.tile([P, 2, BLOCK], F32)
            if rows == BLOCK:
                accs = [psum_acc.tile([P, BLOCK], F32, tag="acc", name="acc%d" % c)[:] for c in range(2)]
            else:
                both = psum_acc.tile([P, 2, rows], F32, tag="acc")
                accs = [both[:, c, :] for c in range(2)]
            for c in HALVES:
                nc.tensor.matmul_mx(
                    out=accs[c],
                    lhsT=w2_words[:, P * c : P * c + P].bitcast(FP8X4),
                    lhsT_scale=w2_scales[:, P * c : P * c + P],
                    rhs=h_codes[:, k, first : first + rows].bitcast(FP8X4),
                    rhs_scale=h_scales[:, k, first : first + rows],
                    start=True,
                    stop=True,
                )
            for c in range(2):
                nc.scalar.activation(
                    out=out_t[:, c, 0:rows], in_=accs[c], func=IDENTITY, bias=cross_bias[:, c : c + 1], scale=1.0
                )
            return out_t

        def flip_and_store(k, first, rows, out_t):
            group, ch = block_of[k]
            chunks = rows // (2 * P)
            c0 = 2 * ch + first // (2 * P)
            result = results.tile([P, 2, 2, EMBED], F32)
            for chunk in range(chunks):
                flipped = psum_flips.tile([P, 2, EMBED], F32, tag="flips")
                for l in range(2):
                    for c in range(2):
                        col = P * (2 * chunk + l)
                        nc.tensor.transpose(
                            out=flipped[:, l, P * c : P * c + P], in_=out_t[:, c, col : col + P], identity=ident[:]
                        )
                nc.scalar.copy(out=result[:, :, chunk, :], in_=flipped[:])
            nc.sync.dma_start(
                out=out_view(group, c0, chunks), in_=result[:, :, 0:chunks, :].rearrange("p l c n -> p l (c n)")
            )

        def direct_matmul(k, chunk):
            acc = psum_direct.tile([P, 2, EMBED], F32, tag="direct")
            for l in range(2):
                first = P * (2 * chunk + l)
                nc.tensor.matmul_mx(
                    out=acc[:, l, :],
                    lhsT=h_codes[:, k, first : first + P].bitcast(FP8X4),
                    lhsT_scale=h_scales[:, k, first : first + P],
                    rhs=w2_words[:].bitcast(FP8X4),
                    rhs_scale=w2_scales[:],
                    start=True,
                    stop=True,
                )
            return acc

        def direct_store(k, chunk, acc):
            group, ch = block_of[k]
            result = results.tile([P, 2, EMBED], F32, name="direct_result")
            nc.vector.tensor_tensor(
                out=result[:],
                in0=cross_row[:].unsqueeze(1).to_broadcast([P, 2, EMBED]),
                in1=acc[:],
                op=ADD,
            )
            nc.sync.dma_start(out=out_view(group, 2 * ch + chunk, 1), in_=result[:])

        VE_GROUPS = [0, 3, 4, 5, 6, 7]
        ve = [(g, ch) for g in VE_GROUPS for ch in range(2)][0:VE_BLOCKS]
        ve[1], ve[2] = ve[2], ve[1]
        gp = [(2, 0), (2, 1), (1, 0), (1, 1), (7, 1)]
        block_of = ve + gp

        def sort_columns(variant, h, rows, cols, dup):
            view = w1_raw[rows, h, :].rearrange("p (q t) -> p t q", t=PACK)
            if dup:
                nc.vector.tensor_copy(
                    out=w1_words[rows, variant, :, :].rearrange("p t (d q) -> p t d q", d=2),
                    in_=view.unsqueeze(2).to_broadcast([HALF, PACK, 2, HALF]),
                )
            else:
                nc.vector.tensor_copy(out=w1_words[rows, variant, :, cols], in_=view)

        low, high = slice(0, HALF), slice(HALF, P)
        tok0 = turn_tokens([0])
        tok1 = turn_tokens([1])
        tok23 = turn_tokens([2, 3])

        sort_columns(2, 1, low, low, False)
        sort_columns(2, 1, high, high, False)
        nc.vector.tensor_copy(
            out=s1[:, :, :, 0:HALF].rearrange("p h t q -> p h q t"),
            in_=s1_raw[:].rearrange("p h (q t) -> p h q t", t=PACK),
        )
        s1_ints = s1[:].rearrange("p h t n -> p (h t n)").bitcast(I32).rearrange("p (k d n) -> p k d n", d=2, n=16)
        nc.vector.tensor_copy(out=s1_ints[:, :, 1, :], in_=s1_ints[:, :, 0, :])
        sort_columns(0, 0, low, None, True)

        banks = {}

        def a_view(group):
            return banks[group][:].rearrange("p t (b l) -> p b l t", l=2)

        unflipped = []

        def flush():
            if unflipped:
                flip_and_store(*unflipped.pop())

        def scalar_out(k, first=0, rows=BLOCK):
            out_t = second_matmul(k, first, rows)
            flush()
            unflipped.append((k, first, rows, out_t))

        quantise_tokens([0], tok0)
        bank0 = b_pass(0)
        banks[0] = a_pass(0)
        quantise_tokens([1], tok1)
        sort_columns(1, 0, high, None, True)
        b_add(0, bank0)
        quantise_tokens([2, 3], tok23)
        bank1 = b_pass(1)
        banks[3] = a_pass(3)
        a_copy(2)
        corr_rows = spread_corr_bias()
        rows2 = b_rows(2)
        rows3 = b_rows(3)
        h_half = half_pool.tile([P, 2 * P, PACK], BF16, align_bytes=64, tag="half")
        add_sets(nc.vector, h_half[:], a_view(0), 0, 2)
        b_add(1, bank1)
        b_turn(2, rows2, corr_rows)
        b_turn(3, rows3, corr_rows)
        quantise(0, h_half[:])
        scalar_out(0, 0, 2 * P)
        h_half = half_pool.tile([P, 2 * P, PACK], BF16, align_bytes=64, tag="half")
        add_sets(nc.vector, h_half[:], a_view(0), 2, 2)
        a_copy(7)
        a_copy(1)
        quantise(2 * P, h_half[:])
        scalar_out(0, 2 * P, 2 * P)

        def gp_half(j):
            group, ch = gp[j // 2]
            h_half = half_pool.tile([P, 2 * P, PACK], BF16, align_bytes=64)
            view = a_sb[:, group, :, :].rearrange("p (b l) t -> p b l t", l=2)
            add_sets(nc.gpsimd, h_half[:], view, SETS * ch + 2 * (j % 2), 2)
            return h_half

        gp_tile = gp_half(0)
        following = {0: 4, 3: 5, 4: 6, 5: 7, 6: None}
        waiting = None
        for i in range(1, VE_BLOCKS):
            group, ch = ve[i]
            h_ve = work.tile([P, BLOCK, PACK], BF16, align_bytes=64)
            add_sets(nc.vector, h_ve[:], a_view(group), SETS * ch, SETS)
            if waiting is not None:
                direct_store(*waiting)
                waiting = None
            j = i - 1
            k_gp = VE_BLOCKS + j // 2
            quantise(BLOCK * k_gp + 2 * P * (j % 2), gp_tile[:])
            quantise(BLOCK * i, h_ve[:])
            if i + 1 < VE_BLOCKS:
                gp_tile = gp_half(i)
                if ch == 1 and following[group] is not None:
                    banks[following[group]] = a_pass(following[group])
            if j >= 10 - DIRECT_HALVES:
                waiting = (k_gp, j % 2, direct_matmul(k_gp, j % 2))
                if j == 10 - DIRECT_HALVES and j % 2 == 1:
                    scalar_out(k_gp, 0, 2 * P)
            elif j % 2 == 1:
                scalar_out(k_gp)
            if i + 1 < VE_BLOCKS:
                scalar_out(i)
            else:
                flush()
                direct_store(*waiting)
                for chunk in range(2):
                    direct_store(i, chunk, direct_matmul(i, chunk))
